import numpy as np
import ml_dtypes


def mxq(x, axis, fmt="e4m3"):
    dtype, down = {"e4m3": (ml_dtypes.float8_e4m3fn, 7), "e5m2": (ml_dtypes.float8_e5m2, 14)}[fmt]
    v = np.moveaxis(np.asarray(x, np.float32).astype(ml_dtypes.bfloat16).astype(np.float64), axis, -1)
    blocks = v.reshape(v.shape[:-1] + (-1, 32))
    amax = np.abs(blocks).max(-1, keepdims=True)
    byte = np.maximum(np.where(amax > 0, np.frexp(amax)[1] - 1 + 127, 0) - down, 1)
    scale = np.exp2(byte - 127.0)
    codes = (blocks / scale).astype(np.float32).astype(dtype).astype(np.float64)
    return np.moveaxis((codes * scale).reshape(v.shape), -1, axis)


WIDE = False


def mx_kscale(k):
    if not WIDE:
        return np.ones(k)
    levels = np.array([10, -10, 5, -5, 0])
    a = np.random.permutation(np.resize(levels, k // 512 * 4)).reshape(k // 512, 4)
    idx = np.arange(k)
    return np.exp2(a[idx // 512, idx % 128 // 32])


BF16 = ml_dtypes.bfloat16


def bf(x):
    return np.asarray(x, np.float32).astype(BF16)


def f64(x):
    return np.asarray(x).astype(np.float64)


B, D, U = 256, 2048, 2048
MASK_DENSITY = 1.0 / 16.0
W_STD = 1.0 / np.sqrt(U * MASK_DENSITY)


def setup_inputs():
    s, t = mx_kscale(U), mx_kscale(U)
    return {"h0": bf(np.random.standard_normal((B, U)) * s),
            "k1": bf(np.random.standard_normal((U, U)) * W_STD / s[:, None] * t),
            "k2": bf(np.random.standard_normal((U, U)) * W_STD / t[:, None]),
            "m1": bf(np.random.random((U, U)) < MASK_DENSITY),
            "m2": bf(np.random.random((U, U)) < MASK_DENSITY),
            "scaling": bf(np.random.uniform(1.25, 1.75, 1)),
            "bias": bf(np.random.standard_normal(U) * 0.5)}


def reference(h0, k1, k2, m1, m2, scaling, bias):
    w1 = f64(k1) * f64(m1)
    w2 = f64(k2) * f64(m2)
    h1 = mxq(f64(h0), 1, "e4m3") @ mxq(w1, 0, "e4m3")
    out = mxq(h1, 1, "e4m3") @ mxq(w2, 0, "e4m3")
    return np.maximum(f64(scaling) * out + f64(bias), 0.0)

@@ -1,0 +1,240 @@
+from contextlib import ExitStack
+
+import concourse.mybir as mybir
+from concourse.masks import make_identity
+
+F32 = mybir.dt.float32
+BF16 = mybir.dt.bfloat16
+U32 = mybir.dt.uint32
+U8 = mybir.dt.uint8
+FP8X4 = mybir.dt.float8_e4m3fn_x4
+ALU = mybir.AluOpType
+ACT = mybir.ActivationFunctionType
+
+P = 128
+B = 256
+U = 2048
+PACK = 4
+KP = P * PACK
+NG = U // KP
+CW = 512
+NC = U // CW
+FLOPS = 2 * 2 * B * U * U
+
+PIN = True
+S_COLS = 400
+HEAD_SPLITS = [(0, 1024), (1024, 2048)]
+TAIL_SPLITS = [(0, 512), (512, 1024), (1024, 1536), (1536, 2048)]
+FULL = [(0, 2048)]
+EVAC_STEPS = [18, 20, 22, 24]
+
+
+def tile_sparsefactorisationdense_pa_kernel(tc, h0, k1, k2, m1, m2, scaling, bias, out):
+    nc = tc.nc
+    with ExitStack() as ctx:
+        const = ctx.enter_context(tc.tile_pool(name="const", bufs=1))
+        raw = ctx.enter_context(tc.tile_pool(name="raw", bufs=3))
+        prd = ctx.enter_context(tc.tile_pool(name="prd", bufs=3))
+        grp = ctx.enter_context(tc.tile_pool(name="grp", bufs=4))
+        hgp = ctx.enter_context(tc.tile_pool(name="hgp", bufs=1))
+        cod = ctx.enter_context(tc.tile_pool(name="cod", bufs=6))
+        outp = ctx.enter_context(tc.tile_pool(name="outp", bufs=4))
+        psum = ctx.enter_context(tc.psum_pool(name="psum", bufs=8))
+        if PIN:
+            ctx.enter_context(tc.manual_schedule())
+
+        raws = {}
+        codes = {}
+        grouped = {}
+
+        def dram_view(x, w, g):
+            rows = x[g * KP:(g + 1) * KP, :]
+            if w == 0:
+                return rows.rearrange("(p j) n -> p j n", j=PACK)
+            return rows.rearrange("(j p) n -> p j n", p=P)
+
+        def load_group(i):
+            w, g = divmod(i, NG)
+            kt = raw.tile([P, PACK * U], BF16, tag="k", name="kt%d" % i)
+            mt = raw.tile([P, PACK * U], BF16, tag="m", name="mt%d" % i)
+            ksrc = dram_view(k1 if w == 0 else k2, w, g)
+            msrc = dram_view(m1 if w == 0 else m2, w, g)
+            splits = HEAD_SPLITS if i == 0 else (TAIL_SPLITS if i == 2 * NG - 1 else FULL)
+            for c0, c1 in splits:
+                kv = kt[:, PACK * c0:PACK * c1].rearrange("p (j n) -> p j n", j=PACK)
+                mv = mt[:, PACK * c0:PACK * c1].rearrange("p (j n) -> p j n", j=PACK)
+                nc.sync.dma_start(out=kv, in_=ksrc[:, :, c0:c1])
+                nc.sync.dma_start(out=mv, in_=msrc[:, :, c0:c1])
+                for c in range(c0 // CW, c1 // CW):
+                    lo = c * CW - c0
+                    raws[i * NC + c] = (kv[:, :, lo:lo + CW], mv[:, :, lo:lo + CW])
+
+        ones = const.tile([P, P], BF16, name="ones")
+        nc.vector.memset(ones[:], 1.0)
+        brow = const.tile([P, U], BF16, name="brow")
+        nc.vector.memset(brow[:], 0.0)
+        ident = const.tile([P, P], F32, name="ident")
+        make_identity(nc, ident[:])
+        nc.scalar.dma_start(out=brow[0:1, :], in_=bias.rearrange("(o n) -> o n", o=1))
+        sc_b = const.tile([P, 1], BF16, name="sc_b")
+        nc.scalar.dma_start(out=sc_b[:], in_=scaling.partition_broadcast(P))
+        sc_f = const.tile([P, 1], F32, name="sc_f")
+
+        load_group(0)
+        h0_sb = const.tile([P, 2 * U], BF16, name="h0_sb")
+        nc.sync.dma_start(out=h0_sb[:].rearrange("p (a k) -> p a k", a=2),
+                          in_=h0.rearrange("(a p) k -> p a k", p=P))
+        load_group(1)
+        load_group(2)
+
+        bias_bc = const.tile([P, U], F32, name="bias_bc")
+        pbs = {}
+        for r in range(NC):
+            pbs[r] = psum.tile([P, CW], F32, tag="bank", name="pb%d" % r)
+            nc.tensor.matmul(out=pbs[r][:], lhsT=ones[:], rhs=brow[:, r * CW:(r + 1) * CW], start=True, stop=True)
+
+        def bias_evac(r):
+            nc.scalar.copy(out=bias_bc[:, r * CW:(r + 1) * CW], in_=pbs[r][:])
+
+        h0w = h0_sb[:].bitcast(F32)
+        h0g = hgp.tile([P, NG * B * PACK], BF16, tag="hg", name="h0g", align_bytes=64)
+        h0gw = h0g[:].bitcast(F32)
+        h0c = const.tile([P, NG, B], U32, name="h0c", align_bytes=64)
+        h0s = const.tile([P, NG, B], U8, name="h0s", align_bytes=64)
+        h0x = {}
+
+        def h0_transpose(g):
+            xt = psum.tile([P, 2 * B], F32, tag="bank", name="xt%d" % g)
+            h0x[g] = xt
+            for u in range(2):
+                for a in range(2):
+                    base = a * (U // 2) + g * (KP // 2)
+                    nc.tensor.transpose(xt[:, u * B + a * P:u * B + (a + 1) * P],
+                                        h0w[:, base + u:base + KP // 2:2], ident[:])
+
+        def h0_evac(g):
+            nc.scalar.copy(out=h0gw[:, g * 2 * B:(g + 1) * 2 * B].rearrange("p (b u) -> p b u", u=2),
+                           in_=h0x[g][:].rearrange("p (u b) -> p b u", u=2))
+
+        def h0_quant(g):
+            nc.vector.quantize_mx(out=h0c[:, g, :].bitcast(FP8X4), scales=h0s[:, g, :],
+                                  in_=h0g[:, g * B * PACK:(g + 1) * B * PACK])
+
+        def stage_a(u):
+            kv, mv = raws[u]
+            pt = prd.tile([P, PACK, CW], BF16, tag="p", name="pt%d" % u)
+            nc.vector.tensor_tensor(out=pt[:], in0=kv, in1=mv, op=ALU.mult)
+            gt = grp.tile([P, CW, PACK], BF16, tag="g", name="gt%d" % u, align_bytes=64)
+            grouped[u] = gt
+            nc.vector.tensor_copy(
+                out=gt[:, S_COLS:CW, :].rearrange("p (c i) t -> p c t i", i=4),
+                in_=pt[:, :, S_COLS:CW].rearrange("p t (c i) -> p c t i", i=4))
+            nc.scalar.copy(
+                out=gt[:, 0:S_COLS, :].rearrange("p (c i) t -> p c t i", i=4),
+                in_=pt[:, :, 0:S_COLS].rearrange("p t (c i) -> p c t i", i=4))
+
+        def stage_b(u):
+            i, c = divmod(u, NC)
+            if c == 0:
+                wc = cod.tile([P, U], U32, tag="wc", name="wc%d" % i, align_bytes=64)
+                ws = cod.tile([P, U], U8, tag="ws", name="ws%d" % i, align_bytes=64)
+                codes[i] = (wc, ws)
+            wc, ws = codes[i]
+            lo = c * CW
+            nc.vector.quantize_mx(out=wc[:, lo:lo + CW].bitcast(FP8X4), scales=ws[:, lo:lo + CW],
+                                  in_=grouped[u][:].rearrange("p c t -> p (c t)"))
+
+        h1t = {}
+        h1c = const.tile([P, NG, B], U32, name="h1c", align_bytes=64)
+        h1s = const.tile([P, NG, B], U8, name="h1s", align_bytes=64)
+        h1p = {}
+
+        def mm1(G):
+            for bh in range(2):
+                h1p[(G, bh)] = psum.tile([P, CW], F32, tag="bank", name="h1p%d_%d" % (G, bh))
+            for t in range(PACK):
+                n0 = G * KP + t * P
+                for g in range(NG):
+                    wc, ws = codes[g]
+                    for bh in range(2):
+                        nc.tensor.matmul_mx(
+                            out=h1p[(G, bh)][:, t * P:(t + 1) * P],
+                            lhsT=wc[:, n0:n0 + P].bitcast(FP8X4), lhsT_scale=ws[:, n0:n0 + P],
+                            rhs=h0c[:, g, bh * P:(bh + 1) * P].bitcast(FP8X4),
+                            rhs_scale=h0s[:, g, bh * P:(bh + 1) * P],
+                            start=(g == 0), stop=(g == NG - 1))
+
+        def h1_evac(G):
+            if G == 0:
+                h1t[0] = hgp.tile([P, NG, B, PACK], BF16, tag="hg", name="h1g", align_bytes=64)
+            for bh in range(2):
+                nc.scalar.copy(out=h1t[0][:, G, bh * P:(bh + 1) * P, :],
+                               in_=h1p[(G, bh)][:].rearrange("p (t b) -> p b t", t=PACK))
+
+        def h1_quant(G):
+            nc.vector.quantize_mx(out=h1c[:, G, :].bitcast(FP8X4), scales=h1s[:, G, :],
+                                  in_=h1t[0][:, G, :, :].rearrange("p b t -> p (b t)"))
+
+        acc = {}
+
+        def mm2(u):
+            i, c = divmod(u, NC)
+            G = i - NG
+            wc, ws = codes[i]
+            lo = c * CW
+            for a in range(2):
+                if G == 0:
+                    acc[(a, c)] = psum.tile([P, CW], F32, tag="bank", name="acc%d_%d" % (a, c))
+                nc.tensor.matmul_mx(
+                    out=acc[(a, c)][:],
+                    lhsT=h1c[:, G, a * P:(a + 1) * P].bitcast(FP8X4), lhsT_scale=h1s[:, G, a * P:(a + 1) * P],
+                    rhs=wc[:, lo:lo + CW].bitcast(FP8X4), rhs_scale=ws[:, lo:lo + CW],
+                    start=(G == 0), stop=(G == NG - 1))
+
+        def epilogue(c):
+            lo = c * CW
+            for a in range(2):
+                o = outp.tile([P, CW], F32, tag="o", name="o%d_%d" % (a, c))
+                nc.vector.scalar_tensor_tensor(out=o[:], in0=acc[(a, c)][:], scalar=sc_f[:, 0:1],
+                                               in1=bias_bc[:, lo:lo + CW], op0=ALU.mult, op1=ALU.add)
+                nc.scalar.activation(out=o[:], in_=o[:], func=ACT.Relu)
+                nc.sync.dma_start(out=out[a * P:(a + 1) * P, lo:lo + CW], in_=o[:])
+
+        NU = 2 * NG * NC
+        pending = []
+        h1_ready = False
+        for g in range(NG):
+            h0_transpose(g)
+        for s in range(NU + 1):
+            if s < NU:
+                stage_a(s)
+                if s % NC == NC - 1 and s // NC + 3 < 2 * NG:
+                    load_group(s // NC + 3)
+            if s >= 1:
+                stage_b(s - 1)
+                if s - 1 == NG * NC - 1:
+                    for G in range(NG):
+                        mm1(G)
+                if s - 1 >= NG * NC:
+                    pending.append(s - 1)
+            if 5 <= s < 5 + NG:
+                h0_evac(s - 5)
+            if 6 <= s < 6 + NG:
+                h0_quant(s - 6)
+            if 10 <= s < 10 + NC:
+                bias_evac(s - 10)
+            if s == 10:
+                nc.vector.tensor_copy(out=sc_f[:], in_=sc_b[:])
+            for G in range(NG):
+                if s == EVAC_STEPS[G]:
+                    h1_evac(G)
+                if s == EVAC_STEPS[G] + 1:
+                    h1_quant(G)
+                    if G == NG - 1:
+                        h1_ready = True
+            if h1_ready:
+                for u in pending:
+                    mm2(u)
+                    if u // NC == 2 * NG - 1:
+                        epilogue(u % NC)
+                pending = []

@@ -19,33 +19,52 @@ KP = P * PACK
 NG = U // KP
 CW = 512
 NC = U // CW
+NGR = 2 * NG
+NU = NGR * NC
 FLOPS = 2 * 2 * B * U * U
 
-PIN = True
-S_COLS = 400
-HEAD_SPLITS = [(0, 1024), (1024, 2048)]
-TAIL_SPLITS = [(0, 512), (512, 1024), (1024, 1536), (1536, 2048)]
-FULL = [(0, 2048)]
-EVAC_STEPS = [18, 20, 22, 24]
+ROWS2 = [("rows", 0, 2), ("rows", 2, 4)]
+QQH = [("cols", 0, 512), ("cols", 512, 1024), ("cols", 1024, 2048)]
+HH = [("cols", 0, 1024), ("cols", 1024, 2048)]
+GROUP_CUTS = [QQH, ROWS2, ROWS2, ROWS2, ROWS2, ROWS2, HH, HH]
+LEAD = 1
+K_BUFS = 4
+M_BUFS = 4
+EVAC0 = 22
+H0_STEP = 5
+
+
+def s_cols(u):
+    if u < 16:
+        return 448
+    if u < 28:
+        return 384
+    return 320
 
 
 def tile_sparsefactorisationdense_pa_kernel(tc, h0, k1, k2, m1, m2, scaling, bias, out):
     nc = tc.nc
     with ExitStack() as ctx:
         const = ctx.enter_context(tc.tile_pool(name="const", bufs=1))
-        raw = ctx.enter_context(tc.tile_pool(name="raw", bufs=3))
-        prd = ctx.enter_context(tc.tile_pool(name="prd", bufs=3))
-        grp = ctx.enter_context(tc.tile_pool(name="grp", bufs=4))
+        kpool = ctx.enter_context(tc.tile_pool(name="kpool", bufs=K_BUFS))
+        mpool = ctx.enter_context(tc.tile_pool(name="mpool", bufs=M_BUFS))
+        grp = ctx.enter_context(tc.tile_pool(name="grp", bufs=6))
         hgp = ctx.enter_context(tc.tile_pool(name="hgp", bufs=1))
         cod = ctx.enter_context(tc.tile_pool(name="cod", bufs=6))
         outp = ctx.enter_context(tc.tile_pool(name="outp", bufs=4))
         psum = ctx.enter_context(tc.psum_pool(name="psum", bufs=8))
-        if PIN:
-            ctx.enter_context(tc.manual_schedule())
+        ctx.enter_context(tc.manual_schedule())
 
-        raws = {}
+        pieces = []
+        for i in range(NGR):
+            for cut in GROUP_CUTS[i]:
+                pieces.append((i, cut[0], cut[1], cut[2]))
+        ktiles = {}
+        unit_src = {}
+        mult_ops = {}
         codes = {}
         grouped = {}
+        state = {"loaded": 0, "mults": 0, "regrouped": 0}
 
         def dram_view(x, w, g):
             rows = x[g * KP:(g + 1) * KP, :]
@@ -53,39 +72,68 @@ def tile_sparsefactorisationdense_pa_kernel(tc, h0, k1, k2, m1, m2, scaling, bia
                 return rows.rearrange("(p j) n -> p j n", j=PACK)
             return rows.rearrange("(j p) n -> p j n", p=P)
 
-        def load_group(i):
+        def load_piece(n):
+            i, kind, a, b = pieces[n]
             w, g = divmod(i, NG)
-            kt = raw.tile([P, PACK * U], BF16, tag="k", name="kt%d" % i)
-            mt = raw.tile([P, PACK * U], BF16, tag="m", name="mt%d" % i)
+            if i not in ktiles:
+                ktiles[i] = kpool.tile([P, PACK * U], BF16, tag="k", name="kt%d" % i)
+            kt = ktiles[i]
+            mt = mpool.tile([P, 2 * U], BF16, tag="m", name="mt%d" % n)
             ksrc = dram_view(k1 if w == 0 else k2, w, g)
             msrc = dram_view(m1 if w == 0 else m2, w, g)
-            splits = HEAD_SPLITS if i == 0 else (TAIL_SPLITS if i == 2 * NG - 1 else FULL)
-            for c0, c1 in splits:
-                kv = kt[:, PACK * c0:PACK * c1].rearrange("p (j n) -> p j n", j=PACK)
-                mv = mt[:, PACK * c0:PACK * c1].rearrange("p (j n) -> p j n", j=PACK)
-                nc.sync.dma_start(out=kv, in_=ksrc[:, :, c0:c1])
-                nc.sync.dma_start(out=mv, in_=msrc[:, :, c0:c1])
-                for c in range(c0 // CW, c1 // CW):
-                    lo = c * CW - c0
-                    raws[i * NC + c] = (kv[:, :, lo:lo + CW], mv[:, :, lo:lo + CW])
+            if kind == "rows":
+                kh = kt[:, a * U:b * U]
+                mh = mt[:, 0:(b - a) * U]
+                nc.sync.dma_start(out=kh.rearrange("p (j n) -> p j n", j=b - a), in_=ksrc[:, a:b, :])
+                nc.sync.dma_start(out=mh.rearrange("p (j n) -> p j n", j=b - a), in_=msrc[:, a:b, :])
+                kv = kt[:].rearrange("p (j n) -> p j n", j=PACK)
+                for c in range(NC):
+                    unit_src[i * NC + c] = kv[:, :, c * CW:(c + 1) * CW]
+            else:
+                kh = kt[:, PACK * a:PACK * b]
+                mh = mt[:, 0:PACK * (b - a)]
+                kv = kh.rearrange("p (j n) -> p j n", j=PACK)
+                nc.sync.dma_start(out=kv, in_=ksrc[:, :, a:b])
+                nc.sync.dma_start(out=mh.rearrange("p (j n) -> p j n", j=PACK), in_=msrc[:, :, a:b])
+                for c in range(a // CW, b // CW):
+                    unit_src[i * NC + c] = kv[:, :, c * CW - a:(c + 1) * CW - a]
+            mult_ops[n] = (kh, mh)
 
-        ones = const.tile([P, P], BF16, name="ones")
-        nc.vector.memset(ones[:], 1.0)
+        def pump_loads():
+            while state["loaded"] < len(pieces):
+                n = state["loaded"]
+                i = pieces[n][0]
+                if n - M_BUFS >= state["mults"]:
+                    return
+                if i not in ktiles and NC * (i - K_BUFS + 1) > state["regrouped"]:
+                    return
+                load_piece(n)
+                state["loaded"] = n + 1
+
+        def mult(n):
+            assert n == state["mults"]
+            kh, mh = mult_ops[n]
+            nc.vector.tensor_tensor(out=kh, in0=kh, in1=mh, op=ALU.mult)
+            state["mults"] = n + 1
+            pump_loads()
+
         brow = const.tile([P, U], BF16, name="brow")
         nc.vector.memset(brow[:], 0.0)
+        ones = const.tile([P, P], BF16, name="ones")
+        nc.vector.memset(ones[:], 1.0)
         ident = const.tile([P, P], F32, name="ident")
         make_identity(nc, ident[:])
-        nc.scalar.dma_start(out=brow[0:1, :], in_=bias.rearrange("(o n) -> o n", o=1))
         sc_b = const.tile([P, 1], BF16, name="sc_b")
-        nc.scalar.dma_start(out=sc_b[:], in_=scaling.partition_broadcast(P))
         sc_f = const.tile([P, 1], F32, name="sc_f")
-
-        load_group(0)
         h0_sb = const.tile([P, 2 * U], BF16, name="h0_sb")
+        for n in range(len(GROUP_CUTS[0])):
+            load_piece(n)
+        state["loaded"] = len(GROUP_CUTS[0])
+        nc.sync.dma_start(out=brow[0:1, :], in_=bias.rearrange("(o n) -> o n", o=1))
+        nc.sync.dma_start(out=sc_b[:], in_=scaling.partition_broadcast(P))
         nc.sync.dma_start(out=h0_sb[:].rearrange("p (a k) -> p a k", a=2),
                           in_=h0.rearrange("(a p) k -> p a k", p=P))
-        load_group(1)
-        load_group(2)
+        pump_loads()
 
         bias_bc = const.tile([P, U], F32, name="bias_bc")
         pbs = {}
@@ -102,14 +150,12 @@ def tile_sparsefactorisationdense_pa_kernel(tc, h0, k1, k2, m1, m2, scaling, bia
         h0c = const.tile([P, NG, B], U32, name="h0c", align_bytes=64)
         h0s = const.tile([P, NG, B], U8, name="h0s", align_bytes=64)
         h0x = {}
-
-        def h0_transpose(g):
-            xt = psum.tile([P, 2 * B], F32, tag="bank", name="xt%d" % g)
-            h0x[g] = xt
+        for g in range(NG):
+            h0x[g] = psum.tile([P, 2 * B], F32, tag="bank", name="xt%d" % g)
             for u in range(2):
                 for a in range(2):
                     base = a * (U // 2) + g * (KP // 2)
-                    nc.tensor.transpose(xt[:, u * B + a * P:u * B + (a + 1) * P],
+                    nc.tensor.transpose(h0x[g][:, u * B + a * P:u * B + (a + 1) * P],
                                         h0w[:, base + u:base + KP // 2:2], ident[:])
 
         def h0_evac(g):
@@ -120,20 +166,21 @@ def tile_sparsefactorisationdense_pa_kernel(tc, h0, k1, k2, m1, m2, scaling, bia
             nc.vector.quantize_mx(out=h0c[:, g, :].bitcast(FP8X4), scales=h0s[:, g, :],
                                   in_=h0g[:, g * B * PACK:(g + 1) * B * PACK])
 
-        def stage_a(u):
-            kv, mv = raws[u]
-            pt = prd.tile([P, PACK, CW], BF16, tag="p", name="pt%d" % u)
-            nc.vector.tensor_tensor(out=pt[:], in0=kv, in1=mv, op=ALU.mult)
+        def regroup(u):
+            src = unit_src[u]
+            sc = s_cols(u)
             gt = grp.tile([P, CW, PACK], BF16, tag="g", name="gt%d" % u, align_bytes=64)
             grouped[u] = gt
-            nc.vector.tensor_copy(
-                out=gt[:, S_COLS:CW, :].rearrange("p (c i) t -> p c t i", i=4),
-                in_=pt[:, :, S_COLS:CW].rearrange("p t (c i) -> p c t i", i=4))
             nc.scalar.copy(
-                out=gt[:, 0:S_COLS, :].rearrange("p (c i) t -> p c t i", i=4),
-                in_=pt[:, :, 0:S_COLS].rearrange("p t (c i) -> p c t i", i=4))
+                out=gt[:, 0:sc, :].rearrange("p (c i) t -> p c t i", i=4),
+                in_=src[:, :, 0:sc].rearrange("p t (c i) -> p c t i", i=4))
+            nc.vector.tensor_copy(
+                out=gt[:, sc:CW, :].rearrange("p (c i) t -> p c t i", i=4),
+                in_=src[:, :, sc:CW].rearrange("p t (c i) -> p c t i", i=4))
+            state["regrouped"] = u + 1
+            pump_loads()
 
-        def stage_b(u):
+        def quantise(u):
             i, c = divmod(u, NC)
             if c == 0:
                 wc = cod.tile([P, U], U32, tag="wc", name="wc%d" % i, align_bytes=64)
@@ -164,12 +211,11 @@ def tile_sparsefactorisationdense_pa_kernel(tc, h0, k1, k2, m1, m2, scaling, bia
                             rhs_scale=h0s[:, g, bh * P:(bh + 1) * P],
                             start=(g == 0), stop=(g == NG - 1))
 
-        def h1_evac(G):
-            if G == 0:
+        def h1_evac(G, bh):
+            if G == 0 and bh == 0:
                 h1t[0] = hgp.tile([P, NG, B, PACK], BF16, tag="hg", name="h1g", align_bytes=64)
-            for bh in range(2):
-                nc.scalar.copy(out=h1t[0][:, G, bh * P:(bh + 1) * P, :],
-                               in_=h1p[(G, bh)][:].rearrange("p (t b) -> p b t", t=PACK))
+            nc.scalar.copy(out=h1t[0][:, G, bh * P:(bh + 1) * P, :],
+                           in_=h1p[(G, bh)][:].rearrange("p (t b) -> p b t", t=PACK))
 
         def h1_quant(G):
             nc.vector.quantize_mx(out=h1c[:, G, :].bitcast(FP8X4), scales=h1s[:, G, :],
@@ -200,41 +246,53 @@ def tile_sparsefactorisationdense_pa_kernel(tc, h0, k1, k2, m1, m2, scaling, bia
                 nc.scalar.activation(out=o[:], in_=o[:], func=ACT.Relu)
                 nc.sync.dma_start(out=out[a * P:(a + 1) * P, lo:lo + CW], in_=o[:])
 
-        NU = 2 * NG * NC
+        mult_at = {}
+        for n in range(len(pieces)):
+            i, kind, a, b = pieces[n]
+            if kind == "rows":
+                s = NC * (i - 1) + a + 1
+            else:
+                s = NC * i + a // CW - LEAD
+            s = max(s, 0)
+            mult_at[s] = mult_at.get(s, []) + [n]
+
         pending = []
-        h1_ready = False
-        for g in range(NG):
-            h0_transpose(g)
+        evacs_done = 0
         for s in range(NU + 1):
+            for n in mult_at.get(s, []):
+                mult(n)
             if s < NU:
-                stage_a(s)
-                if s % NC == NC - 1 and s // NC + 3 < 2 * NG:
-                    load_group(s // NC + 3)
+                regroup(s)
             if s >= 1:
-                stage_b(s - 1)
+                quantise(s - 1)
                 if s - 1 == NG * NC - 1:
                     for G in range(NG):
                         mm1(G)
                 if s - 1 >= NG * NC:
                     pending.append(s - 1)
-            if 5 <= s < 5 + NG:
-                h0_evac(s - 5)
-            if 6 <= s < 6 + NG:
-                h0_quant(s - 6)
-            if 10 <= s < 10 + NC:
-                bias_evac(s - 10)
-            if s == 10:
+            if 1 <= s < 1 + NC:
+                bias_evac(s - 1)
+            if H0_STEP <= s < H0_STEP + NG:
+                h0_evac(s - H0_STEP)
+            if H0_STEP + 1 <= s < H0_STEP + 1 + NG:
+                h0_quant(s - H0_STEP - 1)
+            if s == H0_STEP:
                 nc.vector.tensor_copy(out=sc_f[:], in_=sc_b[:])
-            for G in range(NG):
-                if s == EVAC_STEPS[G]:
-                    h1_evac(G)
-                if s == EVAC_STEPS[G] + 1:
-                    h1_quant(G)
-                    if G == NG - 1:
-                        h1_ready = True
-            if h1_ready:
-                for u in pending:
+            e = s - EVAC0
+            if 0 <= e < 2 * NG:
+                h1_evac(e // 2, e % 2)
+                evacs_done = e + 1
+            if 2 <= e < 2 + 2 * NG and e % 2 == 0:
+                h1_quant(e // 2 - 1)
+            quants_done = max(0, min(NG, e // 2)) if e >= 2 else 0
+            left = []
+            for u in pending:
+                G = u // NC - NG
+                c = u % NC
+                if G < quants_done and evacs_done >= 2 * (c + 1) and not left:
                     mm2(u)
-                    if u // NC == 2 * NG - 1:
-                        epilogue(u % NC)
-                pending = []
+                else:
+                    left.append(u)
+            pending = left
+        for c in range(NC):
+            epilogue(c)

@@ -20,26 +20,33 @@ NG = U // KP
 CW = 512
 NC = U // CW
 NGR = 2 * NG
-NU = NGR * NC
 FLOPS = 2 * 2 * B * U * U
 
 ROWS2 = [("rows", 0, 2), ("rows", 2, 4)]
 QQH = [("cols", 0, 512), ("cols", 512, 1024), ("cols", 1024, 2048)]
 HH = [("cols", 0, 1024), ("cols", 1024, 2048)]
-GROUP_CUTS = [QQH, ROWS2, ROWS2, ROWS2, ROWS2, ROWS2, HH, HH]
+HQQ = [("cols", 0, 1024), ("cols", 1024, 1536), ("cols", 1536, 2048)]
+GROUP_CUTS = [QQH, ROWS2, ROWS2, ROWS2, ROWS2, ROWS2, HH, HQQ]
+SB1 = 704
+SB2 = 576
+GROUP_BLOCKS = [
+    [(0, 512, 448), (512, 1024, 448), (1024, 2048, 896)],
+    [(0, 1024, 1024), (1024, 2048, SB1)],
+    [(0, 1024, 1024), (1024, 2048, SB1)],
+    [(0, 1024, 1024), (1024, 2048, SB1)],
+    [(0, 1024, 1024), (1024, 2048, SB2)],
+    [(0, 1024, 1024), (1024, 2048, SB2)],
+    [(0, 1024, 832), (1024, 2048, 832)],
+    [(0, 1024, 768), (1024, 1536, 320), (1536, 2048, 288)],
+]
 LEAD = 1
 K_BUFS = 4
 M_BUFS = 4
-EVAC0 = 22
+G_BUFS = 4
+H0_AFTER = 6
 H0_STEP = 5
-
-
-def s_cols(u):
-    if u < 16:
-        return 448
-    if u < 28:
-        return 384
-    return 320
+EVAC_STEPS = [10, 11, 12, 13]
+BIAS_STEP = 1
 
 
 def tile_sparsefactorisationdense_pa_kernel(tc, h0, k1, k2, m1, m2, scaling, bias, out):
@@ -48,23 +55,31 @@ def tile_sparsefactorisationdense_pa_kernel(tc, h0, k1, k2, m1, m2, scaling, bia
         const = ctx.enter_context(tc.tile_pool(name="const", bufs=1))
         kpool = ctx.enter_context(tc.tile_pool(name="kpool", bufs=K_BUFS))
         mpool = ctx.enter_context(tc.tile_pool(name="mpool", bufs=M_BUFS))
-        grp = ctx.enter_context(tc.tile_pool(name="grp", bufs=6))
+        grp = ctx.enter_context(tc.tile_pool(name="grp", bufs=G_BUFS))
         hgp = ctx.enter_context(tc.tile_pool(name="hgp", bufs=1))
         cod = ctx.enter_context(tc.tile_pool(name="cod", bufs=6))
-        outp = ctx.enter_context(tc.tile_pool(name="outp", bufs=4))
         psum = ctx.enter_context(tc.psum_pool(name="psum", bufs=8))
         ctx.enter_context(tc.manual_schedule())
 
         pieces = []
+        blocks = []
+        first_block = {}
         for i in range(NGR):
             for cut in GROUP_CUTS[i]:
                 pieces.append((i, cut[0], cut[1], cut[2]))
+            first_block[i] = len(blocks)
+            for blk in GROUP_BLOCKS[i]:
+                blocks.append((i, blk[0], blk[1], blk[2]))
+        first_block[NGR] = len(blocks)
+        NB = len(blocks)
         ktiles = {}
-        unit_src = {}
+        col_src = {}
         mult_ops = {}
         codes = {}
         grouped = {}
         state = {"loaded": 0, "mults": 0, "regrouped": 0}
+
+        h0_sb = hgp.tile([P, 2 * U], BF16, tag="hx", name="h0_sb")
 
         def dram_view(x, w, g):
             rows = x[g * KP:(g + 1) * KP, :]
@@ -86,18 +101,19 @@ def tile_sparsefactorisationdense_pa_kernel(tc, h0, k1, k2, m1, m2, scaling, bia
                 mh = mt[:, 0:(b - a) * U]
                 nc.sync.dma_start(out=kh.rearrange("p (j n) -> p j n", j=b - a), in_=ksrc[:, a:b, :])
                 nc.sync.dma_start(out=mh.rearrange("p (j n) -> p j n", j=b - a), in_=msrc[:, a:b, :])
-                kv = kt[:].rearrange("p (j n) -> p j n", j=PACK)
-                for c in range(NC):
-                    unit_src[i * NC + c] = kv[:, :, c * CW:(c + 1) * CW]
+                col_src[i] = (0, kt[:].rearrange("p (j n) -> p j n", j=PACK))
             else:
                 kh = kt[:, PACK * a:PACK * b]
                 mh = mt[:, 0:PACK * (b - a)]
                 kv = kh.rearrange("p (j n) -> p j n", j=PACK)
                 nc.sync.dma_start(out=kv, in_=ksrc[:, :, a:b])
                 nc.sync.dma_start(out=mh.rearrange("p (j n) -> p j n", j=PACK), in_=msrc[:, :, a:b])
-                for c in range(a // CW, b // CW):
-                    unit_src[i * NC + c] = kv[:, :, c * CW - a:(c + 1) * CW - a]
+                for c in range(a, b, CW):
+                    col_src[(i, c)] = (a, kv)
             mult_ops[n] = (kh, mh)
+            if n + 1 == H0_AFTER:
+                nc.sync.dma_start(out=h0_sb[:].rearrange("p (a k) -> p a k", a=2),
+                                  in_=h0.rearrange("(a p) k -> p a k", p=P))
 
         def pump_loads():
             while state["loaded"] < len(pieces):
@@ -105,7 +121,7 @@ def tile_sparsefactorisationdense_pa_kernel(tc, h0, k1, k2, m1, m2, scaling, bia
                 i = pieces[n][0]
                 if n - M_BUFS >= state["mults"]:
                     return
-                if i not in ktiles and NC * (i - K_BUFS + 1) > state["regrouped"]:
+                if i not in ktiles and i >= K_BUFS and first_block[i - K_BUFS + 1] > state["regrouped"]:
                     return
                 load_piece(n)
                 state["loaded"] = n + 1
@@ -125,14 +141,11 @@ def tile_sparsefactorisationdense_pa_kernel(tc, h0, k1, k2, m1, m2, scaling, bia
         make_identity(nc, ident[:])
         sc_b = const.tile([P, 1], BF16, name="sc_b")
         sc_f = const.tile([P, 1], F32, name="sc_f")
-        h0_sb = const.tile([P, 2 * U], BF16, name="h0_sb")
         for n in range(len(GROUP_CUTS[0])):
             load_piece(n)
         state["loaded"] = len(GROUP_CUTS[0])
         nc.sync.dma_start(out=brow[0:1, :], in_=bias.rearrange("(o n) -> o n", o=1))
         nc.sync.dma_start(out=sc_b[:], in_=scaling.partition_broadcast(P))
-        nc.sync.dma_start(out=h0_sb[:].rearrange("p (a k) -> p a k", a=2),
-                          in_=h0.rearrange("(a p) k -> p a k", p=P))
         pump_loads()
 
         bias_bc = const.tile([P, U], F32, name="bias_bc")
@@ -147,53 +160,54 @@ def tile_sparsefactorisationdense_pa_kernel(tc, h0, k1, k2, m1, m2, scaling, bia
         h0w = h0_sb[:].bitcast(F32)
         h0g = hgp.tile([P, NG * B * PACK], BF16, tag="hg", name="h0g", align_bytes=64)
         h0gw = h0g[:].bitcast(F32)
-        h0c = const.tile([P, NG, B], U32, name="h0c", align_bytes=64)
-        h0s = const.tile([P, NG, B], U8, name="h0s", align_bytes=64)
+        h0c = const.tile([P, NG * B], U32, name="h0c", align_bytes=64)
+        h0s = const.tile([P, NG * B], U8, name="h0s", align_bytes=64)
         h0x = {}
-        for g in range(NG):
+
+        def h0_evac(g):
             h0x[g] = psum.tile([P, 2 * B], F32, tag="bank", name="xt%d" % g)
             for u in range(2):
                 for a in range(2):
                     base = a * (U // 2) + g * (KP // 2)
                     nc.tensor.transpose(h0x[g][:, u * B + a * P:u * B + (a + 1) * P],
                                         h0w[:, base + u:base + KP // 2:2], ident[:])
-
-        def h0_evac(g):
             nc.scalar.copy(out=h0gw[:, g * 2 * B:(g + 1) * 2 * B].rearrange("p (b u) -> p b u", u=2),
                            in_=h0x[g][:].rearrange("p (u b) -> p b u", u=2))
 
-        def h0_quant(g):
-            nc.vector.quantize_mx(out=h0c[:, g, :].bitcast(FP8X4), scales=h0s[:, g, :],
-                                  in_=h0g[:, g * B * PACK:(g + 1) * B * PACK])
+        def h0_quant():
+            nc.vector.quantize_mx(out=h0c[:].bitcast(FP8X4), scales=h0s[:], in_=h0g[:])
 
-        def regroup(u):
-            src = unit_src[u]
-            sc = s_cols(u)
-            gt = grp.tile([P, CW, PACK], BF16, tag="g", name="gt%d" % u, align_bytes=64)
-            grouped[u] = gt
+        def src_view(i, a, b):
+            base, kv = col_src[i] if i in col_src else col_src[(i, a - a % CW)]
+            return kv[:, :, a - base:b - base]
+
+        def regroup(s):
+            i, a, b, sc = blocks[s]
+            gt = grp.tile([P, b - a, PACK], BF16, tag="g", name="gt%d" % s, align_bytes=64)
+            grouped[s] = gt
             nc.scalar.copy(
                 out=gt[:, 0:sc, :].rearrange("p (c i) t -> p c t i", i=4),
-                in_=src[:, :, 0:sc].rearrange("p t (c i) -> p c t i", i=4))
-            nc.vector.tensor_copy(
-                out=gt[:, sc:CW, :].rearrange("p (c i) t -> p c t i", i=4),
-                in_=src[:, :, sc:CW].rearrange("p t (c i) -> p c t i", i=4))
-            state["regrouped"] = u + 1
+                in_=src_view(i, a, a + sc).rearrange("p t (c i) -> p c t i", i=4))
+            if a + sc < b:
+                nc.vector.tensor_copy(
+                    out=gt[:, sc:b - a, :].rearrange("p (c i) t -> p c t i", i=4),
+                    in_=src_view(i, a + sc, b).rearrange("p t (c i) -> p c t i", i=4))
+            state["regrouped"] = s + 1
             pump_loads()
 
-        def quantise(u):
-            i, c = divmod(u, NC)
-            if c == 0:
+        def quantise(s):
+            i, a, b, sc = blocks[s]
+            if a == 0:
                 wc = cod.tile([P, U], U32, tag="wc", name="wc%d" % i, align_bytes=64)
                 ws = cod.tile([P, U], U8, tag="ws", name="ws%d" % i, align_bytes=64)
                 codes[i] = (wc, ws)
             wc, ws = codes[i]
-            lo = c * CW
-            nc.vector.quantize_mx(out=wc[:, lo:lo + CW].bitcast(FP8X4), scales=ws[:, lo:lo + CW],
-                                  in_=grouped[u][:].rearrange("p c t -> p (c t)"))
+            nc.vector.quantize_mx(out=wc[:, a:b].bitcast(FP8X4), scales=ws[:, a:b],
+                                  in_=grouped[s][:].rearrange("p c t -> p (c t)"))
 
-        h1t = {}
-        h1c = const.tile([P, NG, B], U32, name="h1c", align_bytes=64)
-        h1s = const.tile([P, NG, B], U8, name="h1s", align_bytes=64)
+        late = {}
+        h1c = const.tile([P, NG * B], U32, name="h1c", align_bytes=64)
+        h1s = const.tile([P, NG * B], U8, name="h1s", align_bytes=64)
         h1p = {}
 
         def mm1(G):
@@ -204,95 +218,101 @@ def tile_sparsefactorisationdense_pa_kernel(tc, h0, k1, k2, m1, m2, scaling, bia
                 for g in range(NG):
                     wc, ws = codes[g]
                     for bh in range(2):
+                        lo = g * B + bh * P
                         nc.tensor.matmul_mx(
                             out=h1p[(G, bh)][:, t * P:(t + 1) * P],
                             lhsT=wc[:, n0:n0 + P].bitcast(FP8X4), lhsT_scale=ws[:, n0:n0 + P],
-                            rhs=h0c[:, g, bh * P:(bh + 1) * P].bitcast(FP8X4),
-                            rhs_scale=h0s[:, g, bh * P:(bh + 1) * P],
+                            rhs=h0c[:, lo:lo + P].bitcast(FP8X4), rhs_scale=h0s[:, lo:lo + P],
                             start=(g == 0), stop=(g == NG - 1))
 
-        def h1_evac(G, bh):
-            if G == 0 and bh == 0:
-                h1t[0] = hgp.tile([P, NG, B, PACK], BF16, tag="hg", name="h1g", align_bytes=64)
-            nc.scalar.copy(out=h1t[0][:, G, bh * P:(bh + 1) * P, :],
-                           in_=h1p[(G, bh)][:].rearrange("p (t b) -> p b t", t=PACK))
+        def h1_evac(G):
+            if G == 0:
+                late["h1g"] = hgp.tile([P, NG, B, PACK], BF16, tag="hg", name="h1g", align_bytes=64)
+            for bh in range(2):
+                nc.scalar.copy(out=late["h1g"][:, G, bh * P:(bh + 1) * P, :],
+                               in_=h1p[(G, bh)][:].rearrange("p (t b) -> p b t", t=PACK))
 
-        def h1_quant(G):
-            nc.vector.quantize_mx(out=h1c[:, G, :].bitcast(FP8X4), scales=h1s[:, G, :],
-                                  in_=h1t[0][:, G, :, :].rearrange("p b t -> p (b t)"))
+        def h1_quant(G0):
+            nc.vector.quantize_mx(out=h1c[:, G0 * B:(G0 + 2) * B].bitcast(FP8X4), scales=h1s[:, G0 * B:(G0 + 2) * B],
+                                  in_=late["h1g"][:, G0:G0 + 2, :, :].rearrange("p g b t -> p (g b t)"))
 
         acc = {}
 
-        def mm2(u):
-            i, c = divmod(u, NC)
+        def mm2(i, c):
             G = i - NG
             wc, ws = codes[i]
             lo = c * CW
             for a in range(2):
                 if G == 0:
                     acc[(a, c)] = psum.tile([P, CW], F32, tag="bank", name="acc%d_%d" % (a, c))
+                hl = G * B + a * P
                 nc.tensor.matmul_mx(
                     out=acc[(a, c)][:],
-                    lhsT=h1c[:, G, a * P:(a + 1) * P].bitcast(FP8X4), lhsT_scale=h1s[:, G, a * P:(a + 1) * P],
+                    lhsT=h1c[:, hl:hl + P].bitcast(FP8X4), lhsT_scale=h1s[:, hl:hl + P],
                     rhs=wc[:, lo:lo + CW].bitcast(FP8X4), rhs_scale=ws[:, lo:lo + CW],
                     start=(G == 0), stop=(G == NG - 1))
 
         def epilogue(c):
             lo = c * CW
+            if c == 0:
+                late["o0"] = hgp.tile([P, U], F32, tag="hx", name="o_a0")
+                late["o1"] = hgp.tile([P, U], F32, tag="hg", name="o_a1", align_bytes=64)
             for a in range(2):
-                o = outp.tile([P, CW], F32, tag="o", name="o%d_%d" % (a, c))
-                nc.vector.scalar_tensor_tensor(out=o[:], in0=acc[(a, c)][:], scalar=sc_f[:, 0:1],
+                o = late["o%d" % a][:, lo:lo + CW]
+                nc.vector.scalar_tensor_tensor(out=o, in0=acc[(a, c)][:], scalar=sc_f[:, 0:1],
                                                in1=bias_bc[:, lo:lo + CW], op0=ALU.mult, op1=ALU.add)
-                nc.scalar.activation(out=o[:], in_=o[:], func=ACT.Relu)
-                nc.sync.dma_start(out=out[a * P:(a + 1) * P, lo:lo + CW], in_=o[:])
+                nc.scalar.activation(out=o, in_=o, func=ACT.Relu)
+                nc.sync.dma_start(out=out[a * P:(a + 1) * P, lo:lo + CW], in_=o)
 
         mult_at = {}
         for n in range(len(pieces)):
             i, kind, a, b = pieces[n]
             if kind == "rows":
-                s = NC * (i - 1) + a + 1
+                s = first_block[i] - 2 + a // 2
             else:
-                s = NC * i + a // CW - LEAD
+                s = min(x for x in range(NB) if blocks[x][0] == i and blocks[x][1] >= a) - LEAD
             s = max(s, 0)
             mult_at[s] = mult_at.get(s, []) + [n]
 
         pending = []
         evacs_done = 0
-        for s in range(NU + 1):
+        quants_done = 0
+        for s in range(NB + 1):
             for n in mult_at.get(s, []):
                 mult(n)
-            if s < NU:
+            if s < NB:
                 regroup(s)
             if s >= 1:
                 quantise(s - 1)
-                if s - 1 == NG * NC - 1:
+                i, a, b, sc = blocks[s - 1]
+                if s == first_block[NG]:
                     for G in range(NG):
                         mm1(G)
-                if s - 1 >= NG * NC:
-                    pending.append(s - 1)
-            if 1 <= s < 1 + NC:
-                bias_evac(s - 1)
-            if H0_STEP <= s < H0_STEP + NG:
-                h0_evac(s - H0_STEP)
-            if H0_STEP + 1 <= s < H0_STEP + 1 + NG:
-                h0_quant(s - H0_STEP - 1)
-            if s == H0_STEP:
+                if i >= NG:
+                    for c in range(a // CW, b // CW):
+                        pending.append((i, c))
+            if s in (BIAS_STEP, BIAS_STEP + 1):
+                bias_evac(2 * (s - BIAS_STEP))
+                bias_evac(2 * (s - BIAS_STEP) + 1)
+            if s in (H0_STEP, H0_STEP + 1):
+                h0_evac(2 * (s - H0_STEP))
+                h0_evac(2 * (s - H0_STEP) + 1)
+            if s == H0_STEP + 2:
+                h0_quant()
                 nc.vector.tensor_copy(out=sc_f[:], in_=sc_b[:])
-            e = s - EVAC0
-            if 0 <= e < 2 * NG:
-                h1_evac(e // 2, e % 2)
-                evacs_done = e + 1
-            if 2 <= e < 2 + 2 * NG and e % 2 == 0:
-                h1_quant(e // 2 - 1)
-            quants_done = max(0, min(NG, e // 2)) if e >= 2 else 0
+            for G in range(NG):
+                if s == EVAC_STEPS[G]:
+                    h1_evac(G)
+                    evacs_done = 2 * (G + 1)
+                if s == EVAC_STEPS[G] + 1 and G % 2 == 1:
+                    h1_quant(G - 1)
+                    quants_done = G + 1
             left = []
-            for u in pending:
-                G = u // NC - NG
-                c = u % NC
-                if G < quants_done and evacs_done >= 2 * (c + 1) and not left:
-                    mm2(u)
+            for i, c in pending:
+                if i - NG < quants_done and evacs_done >= 2 * (c + 1) and not left:
+                    mm2(i, c)
                 else:
-                    left.append(u)
+                    left.append((i, c))
             pending = left
         for c in range(NC):
             epilogue(c)

@@ -17,302 +17,189 @@ U = 2048
 PACK = 4
 KP = P * PACK
 NG = U // KP
-CW = 512
-NC = U // CW
 NGR = 2 * NG
+BANK = 512
+BLK = 1024
+NBLK = 2 * NGR
 FLOPS = 2 * 2 * B * U * U
 
-ROWS2 = [("rows", 0, 2), ("rows", 2, 4)]
-QQH = [("cols", 0, 512), ("cols", 512, 1024), ("cols", 1024, 2048)]
-HH = [("cols", 0, 1024), ("cols", 1024, 2048)]
-HQQ = [("cols", 0, 1024), ("cols", 1024, 1536), ("cols", 1536, 2048)]
-GROUP_CUTS = [QQH, ROWS2, ROWS2, ROWS2, ROWS2, ROWS2, HH, HQQ]
-SB1 = 704
-SB2 = 576
-GROUP_BLOCKS = [
-    [(0, 512, 448), (512, 1024, 448), (1024, 2048, 896)],
-    [(0, 1024, 1024), (1024, 2048, SB1)],
-    [(0, 1024, 1024), (1024, 2048, SB1)],
-    [(0, 1024, 1024), (1024, 2048, SB1)],
-    [(0, 1024, 1024), (1024, 2048, SB2)],
-    [(0, 1024, 1024), (1024, 2048, SB2)],
-    [(0, 1024, 832), (1024, 2048, 832)],
-    [(0, 1024, 768), (1024, 1536, 320), (1536, 2048, 288)],
-]
-LEAD = 1
-K_BUFS = 4
-M_BUFS = 4
-G_BUFS = 4
-H0_AFTER = 6
-H0_STEP = 5
-EVAC_STEPS = [10, 11, 12, 13]
-BIAS_STEP = 1
+S_SECOND = 640
+S_LAST = (768, 608)
+FIRST_EVAC = NBLK // 2 + 1
 
 
 def tile_sparsefactorisationdense_pa_kernel(tc, h0, k1, k2, m1, m2, scaling, bias, out):
     nc = tc.nc
     with ExitStack() as ctx:
         const = ctx.enter_context(tc.tile_pool(name="const", bufs=1))
-        kpool = ctx.enter_context(tc.tile_pool(name="kpool", bufs=K_BUFS))
-        mpool = ctx.enter_context(tc.tile_pool(name="mpool", bufs=M_BUFS))
-        grp = ctx.enter_context(tc.tile_pool(name="grp", bufs=G_BUFS))
-        hgp = ctx.enter_context(tc.tile_pool(name="hgp", bufs=1))
-        cod = ctx.enter_context(tc.tile_pool(name="cod", bufs=6))
+        kpool = ctx.enter_context(tc.tile_pool(name="kpool", bufs=4))
+        mpool = ctx.enter_context(tc.tile_pool(name="mpool", bufs=4))
+        gpool = ctx.enter_context(tc.tile_pool(name="gpool", bufs=4))
+        reuse = ctx.enter_context(tc.tile_pool(name="reuse", bufs=1))
+        cpool = ctx.enter_context(tc.tile_pool(name="cpool", bufs=6))
         psum = ctx.enter_context(tc.psum_pool(name="psum", bufs=8))
         ctx.enter_context(tc.manual_schedule())
 
-        pieces = []
-        blocks = []
-        first_block = {}
-        for i in range(NGR):
-            for cut in GROUP_CUTS[i]:
-                pieces.append((i, cut[0], cut[1], cut[2]))
-            first_block[i] = len(blocks)
-            for blk in GROUP_BLOCKS[i]:
-                blocks.append((i, blk[0], blk[1], blk[2]))
-        first_block[NGR] = len(blocks)
-        NB = len(blocks)
-        ktiles = {}
-        col_src = {}
-        mult_ops = {}
-        codes = {}
+        products = {}
+        mask_rows = {}
         grouped = {}
-        state = {"loaded": 0, "mults": 0, "regrouped": 0}
+        codes = {}
 
-        h0_sb = hgp.tile([P, 2 * U], BF16, tag="hx", name="h0_sb")
-
-        def dram_view(x, w, g):
-            rows = x[g * KP:(g + 1) * KP, :]
-            if w == 0:
-                return rows.rearrange("(p j) n -> p j n", j=PACK)
-            return rows.rearrange("(j p) n -> p j n", p=P)
-
-        def load_piece(n):
-            i, kind, a, b = pieces[n]
+        def load(i, h):
+            if i >= NGR:
+                return
             w, g = divmod(i, NG)
-            if i not in ktiles:
-                ktiles[i] = kpool.tile([P, PACK * U], BF16, tag="k", name="kt%d" % i)
-            kt = ktiles[i]
-            mt = mpool.tile([P, 2 * U], BF16, tag="m", name="mt%d" % n)
-            ksrc = dram_view(k1 if w == 0 else k2, w, g)
-            msrc = dram_view(m1 if w == 0 else m2, w, g)
-            if kind == "rows":
-                kh = kt[:, a * U:b * U]
-                mh = mt[:, 0:(b - a) * U]
-                nc.sync.dma_start(out=kh.rearrange("p (j n) -> p j n", j=b - a), in_=ksrc[:, a:b, :])
-                nc.sync.dma_start(out=mh.rearrange("p (j n) -> p j n", j=b - a), in_=msrc[:, a:b, :])
-                col_src[i] = (0, kt[:].rearrange("p (j n) -> p j n", j=PACK))
-            else:
-                kh = kt[:, PACK * a:PACK * b]
-                mh = mt[:, 0:PACK * (b - a)]
-                kv = kh.rearrange("p (j n) -> p j n", j=PACK)
-                nc.sync.dma_start(out=kv, in_=ksrc[:, :, a:b])
-                nc.sync.dma_start(out=mh.rearrange("p (j n) -> p j n", j=PACK), in_=msrc[:, :, a:b])
-                for c in range(a, b, CW):
-                    col_src[(i, c)] = (a, kv)
-            mult_ops[n] = (kh, mh)
-            if n + 1 == H0_AFTER:
-                nc.sync.dma_start(out=h0_sb[:].rearrange("p (a k) -> p a k", a=2),
-                                  in_=h0.rearrange("(a p) k -> p a k", p=P))
+            k_rows = (k1, k2)[w][g * KP:(g + 1) * KP, :]
+            m_rows = (m1, m2)[w][g * KP:(g + 1) * KP, :]
+            order = ("(p j) n -> p j n", "(j p) n -> p j n")[w]
+            if h == 0:
+                products[i] = kpool.tile([P, PACK, U], BF16, tag="k", name="k%d" % i)
+            mask_rows[(i, h)] = mpool.tile([P, 2, U], BF16, tag="m", name="m%d_%d" % (i, h))
+            nc.sync.dma_start(out=products[i][:, 2 * h:2 * h + 2, :],
+                              in_=k_rows.rearrange(order, p=P)[:, 2 * h:2 * h + 2, :])
+            nc.sync.dma_start(out=mask_rows[(i, h)][:], in_=m_rows.rearrange(order, p=P)[:, 2 * h:2 * h + 2, :])
 
-        def pump_loads():
-            while state["loaded"] < len(pieces):
-                n = state["loaded"]
-                i = pieces[n][0]
-                if n - M_BUFS >= state["mults"]:
-                    return
-                if i not in ktiles and i >= K_BUFS and first_block[i - K_BUFS + 1] > state["regrouped"]:
-                    return
-                load_piece(n)
-                state["loaded"] = n + 1
+        def multiply(i, h):
+            if i >= NGR:
+                return
+            rows = products[i][:, 2 * h:2 * h + 2, :]
+            nc.vector.tensor_tensor(out=rows, in0=rows, in1=mask_rows[(i, h)][:], op=ALU.mult)
+            load(i + 2, h)
 
-        def mult(n):
-            assert n == state["mults"]
-            kh, mh = mult_ops[n]
-            nc.vector.tensor_tensor(out=kh, in0=kh, in1=mh, op=ALU.mult)
-            state["mults"] = n + 1
-            pump_loads()
+        def regroup(j):
+            i, h = divmod(j, 2)
+            s_cols = S_LAST[h] if i == NGR - 1 else (BLK, S_SECOND)[h]
+            grouped[j] = gpool.tile([P, BLK, PACK], BF16, tag="g", name="g%d" % j, align_bytes=64)
+            src = products[i][:, :, h * BLK:(h + 1) * BLK]
+            nc.scalar.copy(out=grouped[j][:, 0:s_cols, :].rearrange("p (c i) t -> p c t i", i=4),
+                           in_=src[:, :, 0:s_cols].rearrange("p t (c i) -> p c t i", i=4))
+            if s_cols < BLK:
+                nc.vector.tensor_copy(out=grouped[j][:, s_cols:BLK, :].rearrange("p (c i) t -> p c t i", i=4),
+                                      in_=src[:, :, s_cols:BLK].rearrange("p t (c i) -> p c t i", i=4))
 
-        brow = const.tile([P, U], BF16, name="brow")
-        nc.vector.memset(brow[:], 0.0)
+        def quantise(j):
+            i, h = divmod(j, 2)
+            if h == 0:
+                codes[i] = (cpool.tile([P, U], U32, tag="words", name="words%d" % i, align_bytes=64),
+                            cpool.tile([P, U], U8, tag="scales", name="scales%d" % i, align_bytes=64))
+            words, scales = codes[i]
+            cols = slice(h * BLK, (h + 1) * BLK)
+            nc.vector.quantize_mx(out=words[:, cols].bitcast(FP8X4), scales=scales[:, cols],
+                                  in_=grouped[j][:].rearrange("p c t -> p (c t)"))
+
+        h0_sb = reuse.tile([P, 2 * U], BF16, tag="a", name="h0_sb")
+        nc.sync.dma_start(out=h0_sb[:].rearrange("p (a k) -> p a k", a=2), in_=h0.rearrange("(a p) k -> p a k", p=P))
+        bias_row = const.tile([P, U], BF16, name="bias_row")
+        nc.vector.memset(bias_row[:], 0.0)
+        nc.sync.dma_start(out=bias_row[0:1, :], in_=bias.rearrange("(o n) -> o n", o=1))
+        gain_bf = const.tile([P, 1], BF16, name="gain_bf")
+        nc.sync.dma_start(out=gain_bf[:], in_=scaling.partition_broadcast(P))
+        for i in range(2):
+            for h in range(2):
+                load(i, h)
         ones = const.tile([P, P], BF16, name="ones")
         nc.vector.memset(ones[:], 1.0)
         ident = const.tile([P, P], F32, name="ident")
         make_identity(nc, ident[:])
-        sc_b = const.tile([P, 1], BF16, name="sc_b")
-        sc_f = const.tile([P, 1], F32, name="sc_f")
-        for n in range(len(GROUP_CUTS[0])):
-            load_piece(n)
-        state["loaded"] = len(GROUP_CUTS[0])
-        nc.sync.dma_start(out=brow[0:1, :], in_=bias.rearrange("(o n) -> o n", o=1))
-        nc.sync.dma_start(out=sc_b[:], in_=scaling.partition_broadcast(P))
-        pump_loads()
 
-        bias_bc = const.tile([P, U], F32, name="bias_bc")
-        pbs = {}
-        for r in range(NC):
-            pbs[r] = psum.tile([P, CW], F32, tag="bank", name="pb%d" % r)
-            nc.tensor.matmul(out=pbs[r][:], lhsT=ones[:], rhs=brow[:, r * CW:(r + 1) * CW], start=True, stop=True)
+        bias_all = const.tile([P, U], F32, name="bias_all")
+        for c in range(U // BANK):
+            bank = psum.tile([P, BANK], F32, tag="bank", name="bias_ps%d" % c)
+            nc.tensor.matmul(out=bank[:], lhsT=ones[:], rhs=bias_row[:, c * BANK:(c + 1) * BANK], start=True, stop=True)
+            nc.scalar.copy(out=bias_all[:, c * BANK:(c + 1) * BANK], in_=bank[:])
 
-        def bias_evac(r):
-            nc.scalar.copy(out=bias_bc[:, r * CW:(r + 1) * CW], in_=pbs[r][:])
-
-        h0w = h0_sb[:].bitcast(F32)
-        h0g = hgp.tile([P, NG * B * PACK], BF16, tag="hg", name="h0g", align_bytes=64)
-        h0gw = h0g[:].bitcast(F32)
-        h0c = const.tile([P, NG * B], U32, name="h0c", align_bytes=64)
-        h0s = const.tile([P, NG * B], U8, name="h0s", align_bytes=64)
-        h0x = {}
-
-        def h0_evac(g):
-            h0x[g] = psum.tile([P, 2 * B], F32, tag="bank", name="xt%d" % g)
+        h0_words = h0_sb[:].bitcast(F32)
+        h0_grouped = reuse.tile([P, NG * B * PACK], BF16, tag="b", name="h0_grouped", align_bytes=64)
+        h0_codes = const.tile([P, NG * B], U32, name="h0_codes", align_bytes=64)
+        h0_scales = const.tile([P, NG * B], U8, name="h0_scales", align_bytes=64)
+        for g in range(NG):
+            bank = psum.tile([P, 2, B], F32, tag="bank", name="h0_ps%d" % g)
             for u in range(2):
                 for a in range(2):
-                    base = a * (U // 2) + g * (KP // 2)
-                    nc.tensor.transpose(h0x[g][:, u * B + a * P:u * B + (a + 1) * P],
-                                        h0w[:, base + u:base + KP // 2:2], ident[:])
-            nc.scalar.copy(out=h0gw[:, g * 2 * B:(g + 1) * 2 * B].rearrange("p (b u) -> p b u", u=2),
-                           in_=h0x[g][:].rearrange("p (u b) -> p b u", u=2))
+                    first = a * (U // 2) + g * (KP // 2) + u
+                    nc.tensor.transpose(bank[:, u, a * P:(a + 1) * P], h0_words[:, first:first + KP // 2 - 1:2], ident[:])
+            nc.scalar.copy(out=h0_grouped[:].bitcast(F32)[:, g * 2 * B:(g + 1) * 2 * B].rearrange("p (b u) -> p b u", u=2),
+                           in_=bank[:].rearrange("p u b -> p b u"))
+        multiply(0, 0)
+        nc.vector.quantize_mx(out=h0_codes[:].bitcast(FP8X4), scales=h0_scales[:], in_=h0_grouped[:])
+        gain = const.tile([P, 1], F32, name="gain")
+        nc.vector.tensor_copy(out=gain[:], in_=gain_bf[:])
+        multiply(0, 1)
 
-        def h0_quant():
-            nc.vector.quantize_mx(out=h0c[:].bitcast(FP8X4), scales=h0s[:], in_=h0g[:])
-
-        def src_view(i, a, b):
-            base, kv = col_src[i] if i in col_src else col_src[(i, a - a % CW)]
-            return kv[:, :, a - base:b - base]
-
-        def regroup(s):
-            i, a, b, sc = blocks[s]
-            gt = grp.tile([P, b - a, PACK], BF16, tag="g", name="gt%d" % s, align_bytes=64)
-            grouped[s] = gt
-            nc.scalar.copy(
-                out=gt[:, 0:sc, :].rearrange("p (c i) t -> p c t i", i=4),
-                in_=src_view(i, a, a + sc).rearrange("p t (c i) -> p c t i", i=4))
-            if a + sc < b:
-                nc.vector.tensor_copy(
-                    out=gt[:, sc:b - a, :].rearrange("p (c i) t -> p c t i", i=4),
-                    in_=src_view(i, a + sc, b).rearrange("p t (c i) -> p c t i", i=4))
-            state["regrouped"] = s + 1
-            pump_loads()
-
-        def quantise(s):
-            i, a, b, sc = blocks[s]
-            if a == 0:
-                wc = cod.tile([P, U], U32, tag="wc", name="wc%d" % i, align_bytes=64)
-                ws = cod.tile([P, U], U8, tag="ws", name="ws%d" % i, align_bytes=64)
-                codes[i] = (wc, ws)
-            wc, ws = codes[i]
-            nc.vector.quantize_mx(out=wc[:, a:b].bitcast(FP8X4), scales=ws[:, a:b],
-                                  in_=grouped[s][:].rearrange("p c t -> p (c t)"))
-
+        h1_codes = const.tile([P, NG * B], U32, name="h1_codes", align_bytes=64)
+        h1_scales = const.tile([P, NG * B], U8, name="h1_scales", align_bytes=64)
+        h1_banks = {}
         late = {}
-        h1c = const.tile([P, NG * B], U32, name="h1c", align_bytes=64)
-        h1s = const.tile([P, NG * B], U8, name="h1s", align_bytes=64)
-        h1p = {}
-
-        def mm1(G):
-            for bh in range(2):
-                h1p[(G, bh)] = psum.tile([P, CW], F32, tag="bank", name="h1p%d_%d" % (G, bh))
-            for t in range(PACK):
-                n0 = G * KP + t * P
-                for g in range(NG):
-                    wc, ws = codes[g]
-                    for bh in range(2):
-                        lo = g * B + bh * P
-                        nc.tensor.matmul_mx(
-                            out=h1p[(G, bh)][:, t * P:(t + 1) * P],
-                            lhsT=wc[:, n0:n0 + P].bitcast(FP8X4), lhsT_scale=ws[:, n0:n0 + P],
-                            rhs=h0c[:, lo:lo + P].bitcast(FP8X4), rhs_scale=h0s[:, lo:lo + P],
-                            start=(g == 0), stop=(g == NG - 1))
-
-        def h1_evac(G):
-            if G == 0:
-                late["h1g"] = hgp.tile([P, NG, B, PACK], BF16, tag="hg", name="h1g", align_bytes=64)
-            for bh in range(2):
-                nc.scalar.copy(out=late["h1g"][:, G, bh * P:(bh + 1) * P, :],
-                               in_=h1p[(G, bh)][:].rearrange("p (t b) -> p b t", t=PACK))
-
-        def h1_quant(G0):
-            nc.vector.quantize_mx(out=h1c[:, G0 * B:(G0 + 2) * B].bitcast(FP8X4), scales=h1s[:, G0 * B:(G0 + 2) * B],
-                                  in_=late["h1g"][:, G0:G0 + 2, :, :].rearrange("p g b t -> p (g b t)"))
-
         acc = {}
 
-        def mm2(i, c):
-            G = i - NG
-            wc, ws = codes[i]
-            lo = c * CW
-            for a in range(2):
-                if G == 0:
-                    acc[(a, c)] = psum.tile([P, CW], F32, tag="bank", name="acc%d_%d" % (a, c))
-                hl = G * B + a * P
-                nc.tensor.matmul_mx(
-                    out=acc[(a, c)][:],
-                    lhsT=h1c[:, hl:hl + P].bitcast(FP8X4), lhsT_scale=h1s[:, hl:hl + P],
-                    rhs=wc[:, lo:lo + CW].bitcast(FP8X4), rhs_scale=ws[:, lo:lo + CW],
-                    start=(G == 0), stop=(G == NG - 1))
-
-        def epilogue(c):
-            lo = c * CW
-            if c == 0:
-                late["o0"] = hgp.tile([P, U], F32, tag="hx", name="o_a0")
-                late["o1"] = hgp.tile([P, U], F32, tag="hg", name="o_a1", align_bytes=64)
-            for a in range(2):
-                o = late["o%d" % a][:, lo:lo + CW]
-                nc.vector.scalar_tensor_tensor(out=o, in0=acc[(a, c)][:], scalar=sc_f[:, 0:1],
-                                               in1=bias_bc[:, lo:lo + CW], op0=ALU.mult, op1=ALU.add)
-                nc.scalar.activation(out=o, in_=o, func=ACT.Relu)
-                nc.sync.dma_start(out=out[a * P:(a + 1) * P, lo:lo + CW], in_=o)
-
-        mult_at = {}
-        for n in range(len(pieces)):
-            i, kind, a, b = pieces[n]
-            if kind == "rows":
-                s = first_block[i] - 2 + a // 2
-            else:
-                s = min(x for x in range(NB) if blocks[x][0] == i and blocks[x][1] >= a) - LEAD
-            s = max(s, 0)
-            mult_at[s] = mult_at.get(s, []) + [n]
-
-        pending = []
-        evacs_done = 0
-        quants_done = 0
-        for s in range(NB + 1):
-            for n in mult_at.get(s, []):
-                mult(n)
-            if s < NB:
-                regroup(s)
-            if s >= 1:
-                quantise(s - 1)
-                i, a, b, sc = blocks[s - 1]
-                if s == first_block[NG]:
-                    for G in range(NG):
-                        mm1(G)
-                if i >= NG:
-                    for c in range(a // CW, b // CW):
-                        pending.append((i, c))
-            if s in (BIAS_STEP, BIAS_STEP + 1):
-                bias_evac(2 * (s - BIAS_STEP))
-                bias_evac(2 * (s - BIAS_STEP) + 1)
-            if s in (H0_STEP, H0_STEP + 1):
-                h0_evac(2 * (s - H0_STEP))
-                h0_evac(2 * (s - H0_STEP) + 1)
-            if s == H0_STEP + 2:
-                h0_quant()
-                nc.vector.tensor_copy(out=sc_f[:], in_=sc_b[:])
+        def first_product():
             for G in range(NG):
-                if s == EVAC_STEPS[G]:
-                    h1_evac(G)
-                    evacs_done = 2 * (G + 1)
-                if s == EVAC_STEPS[G] + 1 and G % 2 == 1:
-                    h1_quant(G - 1)
-                    quants_done = G + 1
-            left = []
-            for i, c in pending:
-                if i - NG < quants_done and evacs_done >= 2 * (c + 1) and not left:
-                    mm2(i, c)
-                else:
-                    left.append((i, c))
-            pending = left
-        for c in range(NC):
-            epilogue(c)
+                for a in range(2):
+                    h1_banks[(G, a)] = psum.tile([P, PACK, P], F32, tag="bank", name="h1_ps%d_%d" % (G, a))
+                for t in range(PACK):
+                    n0 = G * KP + t * P
+                    for g in range(NG):
+                        words, scales = codes[g]
+                        for a in range(2):
+                            b0 = g * B + a * P
+                            nc.tensor.matmul_mx(out=h1_banks[(G, a)][:, t, :],
+                                                lhsT=words[:, n0:n0 + P].bitcast(FP8X4), lhsT_scale=scales[:, n0:n0 + P],
+                                                rhs=h0_codes[:, b0:b0 + P].bitcast(FP8X4), rhs_scale=h0_scales[:, b0:b0 + P],
+                                                start=(g == 0), stop=(g == NG - 1))
+
+        def empty_h1(G):
+            if G == 0:
+                late["h1"] = reuse.tile([P, NG, B, PACK], BF16, tag="b", name="h1_grouped", align_bytes=64)
+            for a in range(2):
+                nc.scalar.copy(out=late["h1"][:, G, a * P:(a + 1) * P, :], in_=h1_banks[(G, a)][:].rearrange("p t b -> p b t"))
+
+        def quantise_h1(G):
+            nc.vector.quantize_mx(out=h1_codes[:, G * B:(G + 2) * B].bitcast(FP8X4), scales=h1_scales[:, G * B:(G + 2) * B],
+                                  in_=late["h1"][:, G:G + 2, :, :].rearrange("p g b t -> p (g b t)"))
+
+        def second_product(j):
+            i, h = divmod(j, 2)
+            G = i - NG
+            words, scales = codes[i]
+            for c in range(2 * h, 2 * h + 2):
+                for a in range(2):
+                    if G == 0:
+                        acc[(a, c)] = psum.tile([P, BANK], F32, tag="bank", name="acc%d_%d" % (a, c))
+                    b0 = G * B + a * P
+                    nc.tensor.matmul_mx(out=acc[(a, c)][:],
+                                        lhsT=h1_codes[:, b0:b0 + P].bitcast(FP8X4), lhsT_scale=h1_scales[:, b0:b0 + P],
+                                        rhs=words[:, c * BANK:(c + 1) * BANK].bitcast(FP8X4),
+                                        rhs_scale=scales[:, c * BANK:(c + 1) * BANK],
+                                        start=(G == 0), stop=(G == NG - 1))
+
+        waiting = []
+        for j in range(NBLK + 1):
+            i, h = divmod(j, 2)
+            multiply(i + 1, h)
+            if j < NBLK:
+                regroup(j)
+            if j >= 1:
+                quantise(j - 1)
+            if j == NBLK // 2:
+                first_product()
+            if j > NBLK // 2:
+                waiting.append(j - 1)
+            G = j - FIRST_EVAC
+            if 0 <= G < NG:
+                empty_h1(G)
+            if G in (2, 4):
+                quantise_h1(G - 2)
+            if G >= 4:
+                for blk in waiting:
+                    second_product(blk)
+                waiting = []
+
+        staged = (reuse.tile([P, U], F32, tag="a", name="out_a0"),
+                  reuse.tile([P, U], F32, tag="b", name="out_a1", align_bytes=64))
+        for c in range(U // BANK):
+            cols = slice(c * BANK, (c + 1) * BANK)
+            for a in range(2):
+                nc.vector.scalar_tensor_tensor(out=staged[a][:, cols], in0=acc[(a, c)][:], scalar=gain[:, 0:1],
+                                               in1=bias_all[:, cols], op0=ALU.mult, op1=ALU.add)
+                nc.scalar.activation(out=staged[a][:, cols], in_=staged[a][:, cols], func=ACT.Relu)
+                nc.sync.dma_start(out=out[a * P:(a + 1) * P, cols], in_=staged[a][:, cols])

@@ -12,20 +12,19 @@ ALU = mybir.AluOpType
 ACT = mybir.ActivationFunctionType
 
 P = 128
-B = 256
-U = 2048
+BATCH = 256
+WIDTH = 2048
 PACK = 4
-KP = P * PACK
-NG = U // KP
-NGR = 2 * NG
+PASS_ROWS = P * PACK
+PASSES = WIDTH // PASS_ROWS
+GROUPS = 2 * PASSES
+HALF = WIDTH // 2
+STEPS = 2 * GROUPS
 BANK = 512
-BLK = 1024
-NBLK = 2 * NGR
-FLOPS = 2 * 2 * B * U * U
+FLOPS = 2 * 2 * BATCH * WIDTH * WIDTH
 
-S_SECOND = 640
-S_LAST = (768, 608)
-FIRST_EVAC = NBLK // 2 + 1
+SCALAR_COLS = (1024, 640)
+SCALAR_COLS_LAST = (768, 608)
 
 
 def tile_sparsefactorisationdense_pa_kernel(tc, h0, k1, k2, m1, m2, scaling, bias, out):
@@ -35,170 +34,183 @@ def tile_sparsefactorisationdense_pa_kernel(tc, h0, k1, k2, m1, m2, scaling, bia
         kpool = ctx.enter_context(tc.tile_pool(name="kpool", bufs=4))
         mpool = ctx.enter_context(tc.tile_pool(name="mpool", bufs=4))
         gpool = ctx.enter_context(tc.tile_pool(name="gpool", bufs=4))
-        reuse = ctx.enter_context(tc.tile_pool(name="reuse", bufs=1))
+        turns = ctx.enter_context(tc.tile_pool(name="turns", bufs=1))
         cpool = ctx.enter_context(tc.tile_pool(name="cpool", bufs=6))
         psum = ctx.enter_context(tc.psum_pool(name="psum", bufs=8))
         ctx.enter_context(tc.manual_schedule())
 
         products = {}
         mask_rows = {}
-        grouped = {}
+        regrouped = {}
         codes = {}
 
-        def load(i, h):
-            if i >= NGR:
+        def load(group, pair):
+            if group >= GROUPS:
                 return
-            w, g = divmod(i, NG)
-            k_rows = (k1, k2)[w][g * KP:(g + 1) * KP, :]
-            m_rows = (m1, m2)[w][g * KP:(g + 1) * KP, :]
-            order = ("(p j) n -> p j n", "(j p) n -> p j n")[w]
-            if h == 0:
-                products[i] = kpool.tile([P, PACK, U], BF16, tag="k", name="k%d" % i)
-            mask_rows[(i, h)] = mpool.tile([P, 2, U], BF16, tag="m", name="m%d_%d" % (i, h))
-            nc.sync.dma_start(out=products[i][:, 2 * h:2 * h + 2, :],
-                              in_=k_rows.rearrange(order, p=P)[:, 2 * h:2 * h + 2, :])
-            nc.sync.dma_start(out=mask_rows[(i, h)][:], in_=m_rows.rearrange(order, p=P)[:, 2 * h:2 * h + 2, :])
+            weight, g = divmod(group, PASSES)
+            rows = slice(g * PASS_ROWS, (g + 1) * PASS_ROWS)
+            order = ("(p j) n -> p j n", "(j p) n -> p j n")[weight]
+            two = slice(2 * pair, 2 * pair + 2)
+            if pair == 0:
+                products[group] = kpool.tile([P, PACK, WIDTH], BF16, tag="k", name="k%d" % group)
+            mask_rows[(group, pair)] = mpool.tile([P, 2, WIDTH], BF16, tag="m", name="m%d_%d" % (group, pair))
+            nc.sync.dma_start(out=products[group][:, two, :], in_=(k1, k2)[weight][rows, :].rearrange(order, p=P)[:, two, :])
+            nc.sync.dma_start(out=mask_rows[(group, pair)][:], in_=(m1, m2)[weight][rows, :].rearrange(order, p=P)[:, two, :])
 
-        def multiply(i, h):
-            if i >= NGR:
+        def multiply(group, pair):
+            if group >= GROUPS:
                 return
-            rows = products[i][:, 2 * h:2 * h + 2, :]
-            nc.vector.tensor_tensor(out=rows, in0=rows, in1=mask_rows[(i, h)][:], op=ALU.mult)
-            load(i + 2, h)
+            two = products[group][:, 2 * pair:2 * pair + 2, :]
+            nc.vector.tensor_tensor(out=two, in0=two, in1=mask_rows[(group, pair)][:], op=ALU.mult)
+            load(group + 2, pair)
 
-        def regroup(j):
-            i, h = divmod(j, 2)
-            s_cols = S_LAST[h] if i == NGR - 1 else (BLK, S_SECOND)[h]
-            grouped[j] = gpool.tile([P, BLK, PACK], BF16, tag="g", name="g%d" % j, align_bytes=64)
-            src = products[i][:, :, h * BLK:(h + 1) * BLK]
-            nc.scalar.copy(out=grouped[j][:, 0:s_cols, :].rearrange("p (c i) t -> p c t i", i=4),
-                           in_=src[:, :, 0:s_cols].rearrange("p t (c i) -> p c t i", i=4))
-            if s_cols < BLK:
-                nc.vector.tensor_copy(out=grouped[j][:, s_cols:BLK, :].rearrange("p (c i) t -> p c t i", i=4),
-                                      in_=src[:, :, s_cols:BLK].rearrange("p t (c i) -> p c t i", i=4))
+        def regroup(step):
+            group, half = divmod(step, 2)
+            scalar_cols = (SCALAR_COLS_LAST if group == GROUPS - 1 else SCALAR_COLS)[half]
+            regrouped[step] = gpool.tile([P, HALF, PACK], BF16, tag="g", name="g%d" % step, align_bytes=64)
+            src = products[group][:, :, half * HALF:(half + 1) * HALF]
+            nc.scalar.copy(out=regrouped[step][:, 0:scalar_cols, :].rearrange("p (c i) t -> p c t i", i=4),
+                           in_=src[:, :, 0:scalar_cols].rearrange("p t (c i) -> p c t i", i=4))
+            if scalar_cols < HALF:
+                nc.vector.tensor_copy(out=regrouped[step][:, scalar_cols:HALF, :].rearrange("p (c i) t -> p c t i", i=4),
+                                      in_=src[:, :, scalar_cols:HALF].rearrange("p t (c i) -> p c t i", i=4))
 
-        def quantise(j):
-            i, h = divmod(j, 2)
-            if h == 0:
-                codes[i] = (cpool.tile([P, U], U32, tag="words", name="words%d" % i, align_bytes=64),
-                            cpool.tile([P, U], U8, tag="scales", name="scales%d" % i, align_bytes=64))
-            words, scales = codes[i]
-            cols = slice(h * BLK, (h + 1) * BLK)
+        def quantise(step):
+            group, half = divmod(step, 2)
+            if half == 0:
+                codes[group] = (cpool.tile([P, WIDTH], U32, tag="words", name="words%d" % group, align_bytes=64),
+                                cpool.tile([P, WIDTH], U8, tag="scales", name="scales%d" % group, align_bytes=64))
+            words, scales = codes[group]
+            cols = slice(half * HALF, (half + 1) * HALF)
             nc.vector.quantize_mx(out=words[:, cols].bitcast(FP8X4), scales=scales[:, cols],
-                                  in_=grouped[j][:].rearrange("p c t -> p (c t)"))
+                                  in_=regrouped[step][:].rearrange("p c t -> p (c t)"))
 
-        h0_sb = reuse.tile([P, 2 * U], BF16, tag="a", name="h0_sb")
-        nc.sync.dma_start(out=h0_sb[:].rearrange("p (a k) -> p a k", a=2), in_=h0.rearrange("(a p) k -> p a k", p=P))
-        bias_row = const.tile([P, U], BF16, name="bias_row")
+        bias_row = const.tile([P, WIDTH], BF16, name="bias_row")
         nc.vector.memset(bias_row[:], 0.0)
-        nc.sync.dma_start(out=bias_row[0:1, :], in_=bias.rearrange("(o n) -> o n", o=1))
-        gain_bf = const.tile([P, 1], BF16, name="gain_bf")
-        nc.sync.dma_start(out=gain_bf[:], in_=scaling.partition_broadcast(P))
-        for i in range(2):
-            for h in range(2):
-                load(i, h)
         ones = const.tile([P, P], BF16, name="ones")
         nc.vector.memset(ones[:], 1.0)
-        ident = const.tile([P, P], F32, name="ident")
-        make_identity(nc, ident[:])
+        identity = const.tile([P, P], F32, name="identity")
+        make_identity(nc, identity[:])
+        gain_bf16 = const.tile([P, 1], BF16, name="gain_bf16")
+        h0_rows = turns.tile([P, 2 * WIDTH], BF16, tag="a", name="h0_rows")
+        load(0, 0)
+        load(0, 1)
+        nc.sync.dma_start(out=bias_row[0:1, :], in_=bias.rearrange("(o n) -> o n", o=1))
+        nc.sync.dma_start(out=gain_bf16[:], in_=scaling.partition_broadcast(P))
+        nc.sync.dma_start(out=h0_rows[:].rearrange("p (a k) -> p a k", a=2), in_=h0.rearrange("(a p) k -> p a k", p=P))
+        load(1, 0)
+        load(1, 1)
 
-        bias_all = const.tile([P, U], F32, name="bias_all")
-        for c in range(U // BANK):
-            bank = psum.tile([P, BANK], F32, tag="bank", name="bias_ps%d" % c)
-            nc.tensor.matmul(out=bank[:], lhsT=ones[:], rhs=bias_row[:, c * BANK:(c + 1) * BANK], start=True, stop=True)
-            nc.scalar.copy(out=bias_all[:, c * BANK:(c + 1) * BANK], in_=bank[:])
-
-        h0_words = h0_sb[:].bitcast(F32)
-        h0_grouped = reuse.tile([P, NG * B * PACK], BF16, tag="b", name="h0_grouped", align_bytes=64)
-        h0_codes = const.tile([P, NG * B], U32, name="h0_codes", align_bytes=64)
-        h0_scales = const.tile([P, NG * B], U8, name="h0_scales", align_bytes=64)
-        for g in range(NG):
-            bank = psum.tile([P, 2, B], F32, tag="bank", name="h0_ps%d" % g)
-            for u in range(2):
-                for a in range(2):
-                    first = a * (U // 2) + g * (KP // 2) + u
-                    nc.tensor.transpose(bank[:, u, a * P:(a + 1) * P], h0_words[:, first:first + KP // 2 - 1:2], ident[:])
-            nc.scalar.copy(out=h0_grouped[:].bitcast(F32)[:, g * 2 * B:(g + 1) * 2 * B].rearrange("p (b u) -> p b u", u=2),
-                           in_=bank[:].rearrange("p u b -> p b u"))
-        multiply(0, 0)
-        nc.vector.quantize_mx(out=h0_codes[:].bitcast(FP8X4), scales=h0_scales[:], in_=h0_grouped[:])
+        bias_all = const.tile([P, WIDTH], F32, name="bias_all")
         gain = const.tile([P, 1], F32, name="gain")
-        nc.vector.tensor_copy(out=gain[:], in_=gain_bf[:])
-        multiply(0, 1)
+        h0_regrouped = turns.tile([P, PASSES * BATCH * PACK], BF16, tag="b", name="h0_regrouped", align_bytes=64)
+        h0_words = const.tile([P, PASSES * BATCH], U32, name="h0_words", align_bytes=64)
+        h0_scales = const.tile([P, PASSES * BATCH], U8, name="h0_scales", align_bytes=64)
 
-        h1_codes = const.tile([P, NG * B], U32, name="h1_codes", align_bytes=64)
-        h1_scales = const.tile([P, NG * B], U8, name="h1_scales", align_bytes=64)
+        def spread_bias():
+            for c in range(WIDTH // BANK):
+                cols = slice(c * BANK, (c + 1) * BANK)
+                bank = psum.tile([P, BANK], F32, tag="bank", name="bias_bank%d" % c)
+                nc.tensor.matmul(out=bank[:], lhsT=ones[:], rhs=bias_row[:, cols], start=True, stop=True)
+                nc.scalar.copy(out=bias_all[:, cols], in_=bank[:])
+
+        def transpose_h0():
+            as_words = h0_rows[:].bitcast(F32)
+            out_words = h0_regrouped[:].bitcast(F32)
+            for g in range(PASSES):
+                bank = psum.tile([P, 2, BATCH], F32, tag="bank", name="h0_bank%d" % g)
+                for u in range(2):
+                    for a in range(BATCH // P):
+                        first = a * (WIDTH // 2) + g * (PASS_ROWS // 2) + u
+                        nc.tensor.transpose(bank[:, u, a * P:(a + 1) * P], as_words[:, first:first + 2 * P - 1:2], identity[:])
+                nc.scalar.copy(out=out_words[:, g * 2 * BATCH:(g + 1) * 2 * BATCH].rearrange("p (b u) -> p b u", u=2),
+                               in_=bank[:].rearrange("p u b -> p b u"))
+
+        def quantise_h0():
+            nc.vector.quantize_mx(out=h0_words[:].bitcast(FP8X4), scales=h0_scales[:], in_=h0_regrouped[:])
+            nc.vector.tensor_copy(out=gain[:], in_=gain_bf16[:])
+
+        h1_words = const.tile([P, PASSES * BATCH], U32, name="h1_words", align_bytes=64)
+        h1_scales = const.tile([P, PASSES * BATCH], U8, name="h1_scales", align_bytes=64)
         h1_banks = {}
-        late = {}
+        h1_regrouped = {}
         acc = {}
 
         def first_product():
-            for G in range(NG):
-                for a in range(2):
-                    h1_banks[(G, a)] = psum.tile([P, PACK, P], F32, tag="bank", name="h1_ps%d_%d" % (G, a))
+            for G in range(PASSES):
+                for a in range(BATCH // P):
+                    h1_banks[(G, a)] = psum.tile([P, PACK, P], F32, tag="bank", name="h1_bank%d_%d" % (G, a))
                 for t in range(PACK):
-                    n0 = G * KP + t * P
-                    for g in range(NG):
+                    n0 = G * PASS_ROWS + t * P
+                    for g in range(PASSES):
                         words, scales = codes[g]
-                        for a in range(2):
-                            b0 = g * B + a * P
+                        for a in range(BATCH // P):
+                            b0 = g * BATCH + a * P
                             nc.tensor.matmul_mx(out=h1_banks[(G, a)][:, t, :],
                                                 lhsT=words[:, n0:n0 + P].bitcast(FP8X4), lhsT_scale=scales[:, n0:n0 + P],
-                                                rhs=h0_codes[:, b0:b0 + P].bitcast(FP8X4), rhs_scale=h0_scales[:, b0:b0 + P],
-                                                start=(g == 0), stop=(g == NG - 1))
+                                                rhs=h0_words[:, b0:b0 + P].bitcast(FP8X4), rhs_scale=h0_scales[:, b0:b0 + P],
+                                                start=(g == 0), stop=(g == PASSES - 1))
 
         def empty_h1(G):
             if G == 0:
-                late["h1"] = reuse.tile([P, NG, B, PACK], BF16, tag="b", name="h1_grouped", align_bytes=64)
-            for a in range(2):
-                nc.scalar.copy(out=late["h1"][:, G, a * P:(a + 1) * P, :], in_=h1_banks[(G, a)][:].rearrange("p t b -> p b t"))
+                h1_regrouped[0] = turns.tile([P, PASSES, BATCH, PACK], BF16, tag="b", name="h1_regrouped", align_bytes=64)
+            for a in range(BATCH // P):
+                nc.scalar.copy(out=h1_regrouped[0][:, G, a * P:(a + 1) * P, :], in_=h1_banks[(G, a)][:].rearrange("p t b -> p b t"))
 
         def quantise_h1(G):
-            nc.vector.quantize_mx(out=h1_codes[:, G * B:(G + 2) * B].bitcast(FP8X4), scales=h1_scales[:, G * B:(G + 2) * B],
-                                  in_=late["h1"][:, G:G + 2, :, :].rearrange("p g b t -> p (g b t)"))
+            cols = slice(G * BATCH, (G + 2) * BATCH)
+            nc.vector.quantize_mx(out=h1_words[:, cols].bitcast(FP8X4), scales=h1_scales[:, cols],
+                                  in_=h1_regrouped[0][:, G:G + 2, :, :].rearrange("p g b t -> p (g b t)"))
 
-        def second_product(j):
-            i, h = divmod(j, 2)
-            G = i - NG
-            words, scales = codes[i]
-            for c in range(2 * h, 2 * h + 2):
-                for a in range(2):
+        def second_product(step):
+            group, half = divmod(step, 2)
+            G = group - PASSES
+            words, scales = codes[group]
+            for c in range(2 * half, 2 * half + 2):
+                cols = slice(c * BANK, (c + 1) * BANK)
+                for a in range(BATCH // P):
                     if G == 0:
                         acc[(a, c)] = psum.tile([P, BANK], F32, tag="bank", name="acc%d_%d" % (a, c))
-                    b0 = G * B + a * P
+                    b0 = G * BATCH + a * P
                     nc.tensor.matmul_mx(out=acc[(a, c)][:],
-                                        lhsT=h1_codes[:, b0:b0 + P].bitcast(FP8X4), lhsT_scale=h1_scales[:, b0:b0 + P],
-                                        rhs=words[:, c * BANK:(c + 1) * BANK].bitcast(FP8X4),
-                                        rhs_scale=scales[:, c * BANK:(c + 1) * BANK],
-                                        start=(G == 0), stop=(G == NG - 1))
+                                        lhsT=h1_words[:, b0:b0 + P].bitcast(FP8X4), lhsT_scale=h1_scales[:, b0:b0 + P],
+                                        rhs=words[:, cols].bitcast(FP8X4), rhs_scale=scales[:, cols],
+                                        start=(G == 0), stop=(G == PASSES - 1))
 
+        multiply(0, 0)
+        multiply(0, 1)
+        w1_steps = STEPS // 2
         waiting = []
-        for j in range(NBLK + 1):
-            i, h = divmod(j, 2)
-            multiply(i + 1, h)
-            if j < NBLK:
-                regroup(j)
-            if j >= 1:
-                quantise(j - 1)
-            if j == NBLK // 2:
+        for step in range(STEPS + 1):
+            multiply(step // 2 + 1, step % 2)
+            if step < STEPS:
+                regroup(step)
+            if step >= 1:
+                quantise(step - 1)
+            if step > w1_steps:
+                waiting.append(step - 1)
+            if step == 1:
+                spread_bias()
+                transpose_h0()
+            if step == 2:
+                quantise_h0()
+            if step == w1_steps:
                 first_product()
-            if j > NBLK // 2:
-                waiting.append(j - 1)
-            G = j - FIRST_EVAC
-            if 0 <= G < NG:
+            G = step - w1_steps - 1
+            if 0 <= G < PASSES:
                 empty_h1(G)
             if G in (2, 4):
                 quantise_h1(G - 2)
-            if G >= 4:
-                for blk in waiting:
-                    second_product(blk)
+            if G >= PASSES:
+                for earlier in waiting:
+                    second_product(earlier)
                 waiting = []
 
-        staged = (reuse.tile([P, U], F32, tag="a", name="out_a0"),
-                  reuse.tile([P, U], F32, tag="b", name="out_a1", align_bytes=64))
-        for c in range(U // BANK):
+        staged = (turns.tile([P, WIDTH], F32, tag="a", name="out_rows0"),
+                  turns.tile([P, WIDTH], F32, tag="b", name="out_rows1", align_bytes=64))
+        for c in range(WIDTH // BANK):
             cols = slice(c * BANK, (c + 1) * BANK)
-            for a in range(2):
+            for a in range(BATCH // P):
                 nc.vector.scalar_tensor_tensor(out=staged[a][:, cols], in0=acc[(a, c)][:], scalar=gain[:, 0:1],
                                                in1=bias_all[:, cols], op0=ALU.mult, op1=ALU.add)
                 nc.scalar.activation(out=staged[a][:, cols], in_=staged[a][:, cols], func=ACT.Relu)

from contextlib import ExitStack

import concourse.mybir as mybir
from concourse.masks import make_identity

F32 = mybir.dt.float32
BF16 = mybir.dt.bfloat16
U32 = mybir.dt.uint32
U8 = mybir.dt.uint8
FP8X4 = mybir.dt.float8_e4m3fn_x4
ALU = mybir.AluOpType
ACT = mybir.ActivationFunctionType

P = 128
BATCH = 256
WIDTH = 2048
PACK = 4
PASS_ROWS = P * PACK
PASSES = WIDTH // PASS_ROWS
GROUPS = 2 * PASSES
HALF = WIDTH // 2
STEPS = 2 * GROUPS
BANK = 512
FLOPS = 2 * 2 * BATCH * WIDTH * WIDTH

SCALAR_COLS = (1024, 640)
SCALAR_COLS_LAST = (768, 608)


def tile_sparsefactorisationdense_pa_kernel(tc, h0, k1, k2, m1, m2, scaling, bias, out):
    nc = tc.nc
    with ExitStack() as ctx:
        const = ctx.enter_context(tc.tile_pool(name="const", bufs=1))
        kpool = ctx.enter_context(tc.tile_pool(name="kpool", bufs=4))
        mpool = ctx.enter_context(tc.tile_pool(name="mpool", bufs=4))
        gpool = ctx.enter_context(tc.tile_pool(name="gpool", bufs=4))
        turns = ctx.enter_context(tc.tile_pool(name="turns", bufs=1))
        cpool = ctx.enter_context(tc.tile_pool(name="cpool", bufs=6))
        psum = ctx.enter_context(tc.psum_pool(name="psum", bufs=8))
        ctx.enter_context(tc.manual_schedule())

        products = {}
        mask_rows = {}
        regrouped = {}
        codes = {}

        def load(group, pair):
            if group >= GROUPS:
                return
            weight, g = divmod(group, PASSES)
            rows = slice(g * PASS_ROWS, (g + 1) * PASS_ROWS)
            order = ("(p j) n -> p j n", "(j p) n -> p j n")[weight]
            two = slice(2 * pair, 2 * pair + 2)
            if pair == 0:
                products[group] = kpool.tile([P, PACK, WIDTH], BF16, tag="k", name="k%d" % group)
            mask_rows[(group, pair)] = mpool.tile([P, 2, WIDTH], BF16, tag="m", name="m%d_%d" % (group, pair))
            nc.sync.dma_start(out=products[group][:, two, :], in_=(k1, k2)[weight][rows, :].rearrange(order, p=P)[:, two, :])
            nc.sync.dma_start(out=mask_rows[(group, pair)][:], in_=(m1, m2)[weight][rows, :].rearrange(order, p=P)[:, two, :])

        def multiply(group, pair):
            if group >= GROUPS:
                return
            two = products[group][:, 2 * pair:2 * pair + 2, :]
            nc.vector.tensor_tensor(out=two, in0=two, in1=mask_rows[(group, pair)][:], op=ALU.mult)
            load(group + 2, pair)

        def regroup(step):
            group, half = divmod(step, 2)
            scalar_cols = (SCALAR_COLS_LAST if group == GROUPS - 1 else SCALAR_COLS)[half]
            regrouped[step] = gpool.tile([P, HALF, PACK], BF16, tag="g", name="g%d" % step, align_bytes=64)
            src = products[group][:, :, half * HALF:(half + 1) * HALF]
            nc.scalar.copy(out=regrouped[step][:, 0:scalar_cols, :].rearrange("p (c i) t -> p c t i", i=4),
                           in_=src[:, :, 0:scalar_cols].rearrange("p t (c i) -> p c t i", i=4))
            if scalar_cols < HALF:
                nc.vector.tensor_copy(out=regrouped[step][:, scalar_cols:HALF, :].rearrange("p (c i) t -> p c t i", i=4),
                                      in_=src[:, :, scalar_cols:HALF].rearrange("p t (c i) -> p c t i", i=4))

        def quantise(step):
            group, half = divmod(step, 2)
            if half == 0:
                codes[group] = (cpool.tile([P, WIDTH], U32, tag="words", name="words%d" % group, align_bytes=64),
                                cpool.tile([P, WIDTH], U8, tag="scales", name="scales%d" % group, align_bytes=64))
            words, scales = codes[group]
            cols = slice(half * HALF, (half + 1) * HALF)
            nc.vector.quantize_mx(out=words[:, cols].bitcast(FP8X4), scales=scales[:, cols],
                                  in_=regrouped[step][:].rearrange("p c t -> p (c t)"))

        bias_row = const.tile([P, WIDTH], BF16, name="bias_row")
        nc.vector.memset(bias_row[:], 0.0)
        ones = const.tile([P, P], BF16, name="ones")
        nc.vector.memset(ones[:], 1.0)
        identity = const.tile([P, P], F32, name="identity")
        make_identity(nc, identity[:])
        gain_bf16 = const.tile([P, 1], BF16, name="gain_bf16")
        h0_rows = turns.tile([P, 2 * WIDTH], BF16, tag="a", name="h0_rows")
        load(0, 0)
        load(0, 1)
        nc.sync.dma_start(out=bias_row[0:1, :], in_=bias.rearrange("(o n) -> o n", o=1))
        nc.sync.dma_start(out=gain_bf16[:], in_=scaling.partition_broadcast(P))
        nc.sync.dma_start(out=h0_rows[:].rearrange("p (a k) -> p a k", a=2), in_=h0.rearrange("(a p) k -> p a k", p=P))
        load(1, 0)
        load(1, 1)

        bias_all = const.tile([P, WIDTH], F32, name="bias_all")
        gain = const.tile([P, 1], F32, name="gain")
        h0_regrouped = turns.tile([P, PASSES * BATCH * PACK], BF16, tag="b", name="h0_regrouped", align_bytes=64)
        h0_words = const.tile([P, PASSES * BATCH], U32, name="h0_words", align_bytes=64)
        h0_scales = const.tile([P, PASSES * BATCH], U8, name="h0_scales", align_bytes=64)

        def spread_bias():
            for c in range(WIDTH // BANK):
                cols = slice(c * BANK, (c + 1) * BANK)
                bank = psum.tile([P, BANK], F32, tag="bank", name="bias_bank%d" % c)
                nc.tensor.matmul(out=bank[:], lhsT=ones[:], rhs=bias_row[:, cols], start=True, stop=True)
                nc.scalar.copy(out=bias_all[:, cols], in_=bank[:])

        def transpose_h0():
            as_words = h0_rows[:].bitcast(F32)
            out_words = h0_regrouped[:].bitcast(F32)
            for g in range(PASSES):
                bank = psum.tile([P, 2, BATCH], F32, tag="bank", name="h0_bank%d" % g)
                for u in range(2):
                    for a in range(BATCH // P):
                        first = a * (WIDTH // 2) + g * (PASS_ROWS // 2) + u
                        nc.tensor.transpose(bank[:, u, a * P:(a + 1) * P], as_words[:, first:first + 2 * P - 1:2], identity[:])
                nc.scalar.copy(out=out_words[:, g * 2 * BATCH:(g + 1) * 2 * BATCH].rearrange("p (b u) -> p b u", u=2),
                               in_=bank[:].rearrange("p u b -> p b u"))

        def quantise_h0():
            nc.vector.quantize_mx(out=h0_words[:].bitcast(FP8X4), scales=h0_scales[:], in_=h0_regrouped[:])
            nc.vector.tensor_copy(out=gain[:], in_=gain_bf16[:])

        h1_words = const.tile([P, PASSES * BATCH], U32, name="h1_words", align_bytes=64)
        h1_scales = const.tile([P, PASSES * BATCH], U8, name="h1_scales", align_bytes=64)
        h1_banks = {}
        h1_regrouped = {}
        acc = {}

        def first_product():
            for G in range(PASSES):
                for a in range(BATCH // P):
                    h1_banks[(G, a)] = psum.tile([P, PACK, P], F32, tag="bank", name="h1_bank%d_%d" % (G, a))
                for t in range(PACK):
                    n0 = G * PASS_ROWS + t * P
                    for g in range(PASSES):
                        words, scales = codes[g]
                        for a in range(BATCH // P):
                            b0 = g * BATCH + a * P
                            nc.tensor.matmul_mx(out=h1_banks[(G, a)][:, t, :],
                                                lhsT=words[:, n0:n0 + P].bitcast(FP8X4), lhsT_scale=scales[:, n0:n0 + P],
                                                rhs=h0_words[:, b0:b0 + P].bitcast(FP8X4), rhs_scale=h0_scales[:, b0:b0 + P],
                                                start=(g == 0), stop=(g == PASSES - 1))

        def empty_h1(G):
            if G == 0:
                h1_regrouped[0] = turns.tile([P, PASSES, BATCH, PACK], BF16, tag="b", name="h1_regrouped", align_bytes=64)
            for a in range(BATCH // P):
                nc.scalar.copy(out=h1_regrouped[0][:, G, a * P:(a + 1) * P, :], in_=h1_banks[(G, a)][:].rearrange("p t b -> p b t"))

        def quantise_h1(G):
            cols = slice(G * BATCH, (G + 2) * BATCH)
            nc.vector.quantize_mx(out=h1_words[:, cols].bitcast(FP8X4), scales=h1_scales[:, cols],
                                  in_=h1_regrouped[0][:, G:G + 2, :, :].rearrange("p g b t -> p (g b t)"))

        def second_product(step):
            group, half = divmod(step, 2)
            G = group - PASSES
            words, scales = codes[group]
            for c in range(2 * half, 2 * half + 2):
                cols = slice(c * BANK, (c + 1) * BANK)
                for a in range(BATCH // P):
                    if G == 0:
                        acc[(a, c)] = psum.tile([P, BANK], F32, tag="bank", name="acc%d_%d" % (a, c))
                    b0 = G * BATCH + a * P
                    nc.tensor.matmul_mx(out=acc[(a, c)][:],
                                        lhsT=h1_words[:, b0:b0 + P].bitcast(FP8X4), lhsT_scale=h1_scales[:, b0:b0 + P],
                                        rhs=words[:, cols].bitcast(FP8X4), rhs_scale=scales[:, cols],
                                        start=(G == 0), stop=(G == PASSES - 1))

        multiply(0, 0)
        multiply(0, 1)
        w1_steps = STEPS // 2
        waiting = []
        for step in range(STEPS + 1):
            multiply(step // 2 + 1, step % 2)
            if step < STEPS:
                regroup(step)
            if step >= 1:
                quantise(step - 1)
            if step > w1_steps:
                waiting.append(step - 1)
            if step == 1:
                spread_bias()
                transpose_h0()
            if step == 2:
                quantise_h0()
            if step == w1_steps:
                first_product()
            G = step - w1_steps - 1
            if 0 <= G < PASSES:
                empty_h1(G)
            if G in (2, 4):
                quantise_h1(G - 2)
            if G >= PASSES:
                for earlier in waiting:
                    second_product(earlier)
                waiting = []

        staged = (turns.tile([P, WIDTH], F32, tag="a", name="out_rows0"),
                  turns.tile([P, WIDTH], F32, tag="b", name="out_rows1", align_bytes=64))
        for c in range(WIDTH // BANK):
            cols = slice(c * BANK, (c + 1) * BANK)
            for a in range(BATCH // P):
                nc.vector.scalar_tensor_tensor(out=staged[a][:, cols], in0=acc[(a, c)][:], scalar=gain[:, 0:1],
                                               in1=bias_all[:, cols], op0=ALU.mult, op1=ALU.add)
                nc.scalar.activation(out=staged[a][:, cols], in_=staged[a][:, cols], func=ACT.Relu)
                nc.sync.dma_start(out=out[a * P:(a + 1) * P, cols], in_=staged[a][:, cols])
